import numpy as np
import ml_dtypes


def mxq(x, axis, fmt="e4m3"):
    dtype, down = {"e4m3": (ml_dtypes.float8_e4m3fn, 7), "e5m2": (ml_dtypes.float8_e5m2, 14)}[fmt]
    v = np.moveaxis(np.asarray(x, np.float32).astype(ml_dtypes.bfloat16).astype(np.float64), axis, -1)
    blocks = v.reshape(v.shape[:-1] + (-1, 32))
    amax = np.abs(blocks).max(-1, keepdims=True)
    byte = np.maximum(np.where(amax > 0, np.frexp(amax)[1] - 1 + 127, 0) - down, 1)
    scale = np.exp2(byte - 127.0)
    codes = (blocks / scale).astype(np.float32).astype(dtype).astype(np.float64)
    return np.moveaxis((codes * scale).reshape(v.shape), -1, axis)


WIDE = False


def mx_kscale(k):
    if not WIDE:
        return np.ones(k)
    levels = np.array([10, -10, 5, -5, 0])
    a = np.random.permutation(np.resize(levels, k // 512 * 4)).reshape(k // 512, 4)
    idx = np.arange(k)
    return np.exp2(a[idx // 512, idx % 128 // 32])


BF16 = ml_dtypes.bfloat16


def bf(x):
    return np.asarray(x, np.float32).astype(BF16)


def f64(x):
    return np.asarray(x).astype(np.float64)


B, I, H, C, S = 1024, 512, 1024, 511, 3
EPSILON = 1e-6
CC = 1 + C
K = I + H


def setup_inputs():
    s = mx_kscale(K)
    t = mx_kscale(CC)
    t = t / t.min()
    return {
        "invariant_input": bf(np.random.standard_normal((B, I)) * s[:I]),
        "equivariant_input": bf(np.random.standard_normal((B, S)) * 0.125 * t[0]),
        "invariant_hidden": bf(np.random.standard_normal((B, H)) * s[I:]),
        "equivariant_hidden": bf(np.random.standard_normal((B, S, C)) * 0.125 * t[1:]),
        "W_left": bf(np.random.standard_normal((CC, H)) * 0.15 / np.sqrt(CC) * t[:, None]),
        "W_right": bf(np.random.standard_normal((CC, H)) * 0.15 / np.sqrt(CC) * t[:, None]),
        "W_ii": bf(np.random.standard_normal((K, H)) * 0.6 / np.sqrt(K) / s[:, None]),
        "b_ii": bf(np.random.standard_normal(H) * 0.3),
    }


def reference(invariant_input, equivariant_input, invariant_hidden, equivariant_hidden, W_left, W_right, W_ii, b_ii):
    eq_comb = np.concatenate([f64(equivariant_input)[..., None], f64(equivariant_hidden)], axis=-1)
    inv_comb = np.concatenate([f64(invariant_input), f64(invariant_hidden)], axis=-1)
    norm = np.sum(eq_comb * eq_comb, axis=-2, keepdims=True) + EPSILON
    xn = mxq(eq_comb / norm, 2, "e4m3")
    left = xn @ mxq(f64(W_left), 0, "e4m3")
    right = xn @ mxq(f64(W_right), 0, "e4m3")
    proj = np.sum(left * right, axis=-2)
    lin = mxq(inv_comb, 1, "e4m3") @ mxq(f64(W_ii), 0, "e4m3")
    return np.tanh(proj + lin + f64(b_ii))

@@ -1,0 +1,283 @@
+from contextlib import ExitStack
+
+import concourse.mybir as mybir
+from concourse.masks import make_identity
+
+F32 = mybir.dt.float32
+BF16 = mybir.dt.bfloat16
+U32 = mybir.dt.uint32
+U8 = mybir.dt.uint8
+FP8X4 = mybir.dt.float8_e4m3fn_x4
+ACT = mybir.ActivationFunctionType
+ALU = mybir.AluOpType
+
+FLOPS = 2 * (2 * 3072 * 512 * 1024 + 1024 * 1536 * 1024)
+EPS = 1e-6
+P = 128
+WR, WL, WI = 0, 1, 2
+ORDER = (
+    ("le", 0), ("hd", 0), ("lw", 1, 0), ("le", 1), ("le", 2), ("e1", 0), ("lw", 0, 0), ("hd", 1),
+    ("sq", 0, 0), ("sq", 0, 2), ("sq", 0, 1), ("e1", 1), ("wr", 1, 0, "v"), ("lw", 2, 0), ("hd", 2),
+    ("ea", 0, 2, "g"), ("ea", 0, 1, "v"), ("lw", 4, 0), ("wr", 0, 0, "v"), ("wq", 0, 0), ("lw", 3, 0),
+    ("sq", 1, 0), ("rs", 0), ("sy", 0), ("li", 0), ("sq", 1, 1), ("wq", 1, 0), ("sq", 1, 2),
+    ("wr", 2, 0, "s"), ("e2", 0), ("xm", 0, 0), ("xm", 0, 1), ("lw", 2, 1), ("xm", 0, 2), ("xq", 0, 1),
+    ("xq", 0, 0), ("ea", 1, 1, "g"), ("le", 3), ("ea", 1, 2, "g"), ("lw", 1, 1), ("xq", 0, 2), ("it", 0),
+    ("wq", 2, 0), ("li", 1), ("ic", 0, 2, "s"), ("iq", 0, 2), ("lr", 0, 0, 0), ("ic", 0, 0, "s"), ("li", 2),
+    ("ic", 0, 1, "v"), ("rs", 1), ("sy", 1), ("wr", 3, 0, "v"), ("e1", 2), ("sq", 2, 0), ("iq", 0, 1),
+    ("wr", 4, 0, "v"), ("wq", 3, 0), ("lr", 0, 0, 1), ("sq", 2, 2), ("wq", 4, 0), ("lw", 0, 1), ("iq", 0, 0),
+    ("sq", 2, 1), ("lw", 3, 1), ("wr", 0, 1, "v"), ("lr", 0, 0, 2), ("hd", 3), ("wr", 1, 1, "s"), ("it", 1),
+    ("ic", 1, 1, "s"), ("wq", 0, 1), ("pa", 0, 0, 1, "g"), ("ln", 0, 0), ("ic", 1, 0, "s"), ("wq", 1, 1),
+    ("pa", 0, 0, 2, "g"), ("wr", 2, 1, "v"), ("lr", 0, 1, 2), ("iq", 1, 0), ("wq", 2, 1), ("ic", 1, 2, "s"),
+    ("li", 3), ("lw", 4, 1), ("ea", 2, 2, "g"), ("lr", 0, 1, 0), ("e2", 1), ("wr", 4, 1, "s"),
+    ("la", 0, 0, "g"), ("iq", 1, 2), ("xm", 1, 0), ("xm", 1, 1), ("iq", 1, 1), ("xq", 1, 0),
+    ("wr", 3, 1, "s"), ("wq", 3, 1), ("ea", 2, 1, "g"), ("pa", 0, 1, 2, "g"), ("wq", 4, 1), ("lr", 0, 1, 1),
+    ("xq", 1, 1), ("rs", 2), ("sy", 2), ("ln", 0, 1), ("lr", 1, 0, 1), ("xm", 1, 2), ("pa", 0, 1, 1, "g"),
+    ("xq", 1, 2), ("lr", 1, 0, 0), ("e1", 3), ("sq", 3, 0), ("pa", 1, 0, 1, "v"), ("sq", 3, 1),
+    ("la", 0, 1, "g"), ("lr", 1, 0, 2), ("sq", 3, 2), ("ea", 3, 1, "v"), ("ea", 3, 2, "g"), ("lr", 1, 1, 0),
+    ("it", 2), ("ic", 2, 1, "s"), ("pa", 1, 0, 2, "g"), ("ln", 1, 0), ("ic", 2, 2, "s"), ("ic", 2, 0, "s"),
+    ("iq", 2, 0), ("rs", 3), ("iq", 2, 2), ("e2", 2), ("xm", 2, 0), ("xq", 2, 0), ("iq", 2, 1),
+    ("lr", 1, 1, 1), ("lr", 1, 1, 2), ("xm", 2, 2), ("la", 1, 0, "g"), ("xm", 2, 1), ("th", 0, 1),
+    ("pa", 1, 1, 2, "g"), ("ln", 2, 0), ("ln", 1, 1), ("xq", 2, 1), ("pa", 1, 1, 1, "g"), ("it", 3),
+    ("th", 0, 0), ("la", 1, 1, "g"), ("xq", 2, 2), ("lr", 2, 0, 0), ("lr", 2, 0, 2), ("lr", 2, 0, 1),
+    ("lr", 2, 1, 0), ("ic", 3, 2, "v"), ("ic", 3, 0, "s"), ("sy", 3), ("pa", 2, 0, 2, "g"),
+    ("ic", 3, 1, "s"), ("e2", 3), ("iq", 3, 2), ("th", 1, 1), ("pa", 2, 0, 1, "g"), ("iq", 3, 0),
+    ("xm", 3, 0), ("xq", 3, 0), ("xm", 3, 1), ("th", 1, 0), ("la", 2, 0, "g"), ("xm", 3, 2), ("lr", 2, 1, 2),
+    ("pa", 2, 1, 2, "g"), ("lr", 2, 1, 1), ("xq", 3, 1), ("pa", 2, 1, 1, "g"), ("ln", 2, 1), ("xq", 3, 2),
+    ("lr", 3, 0, 0), ("lr", 3, 0, 1), ("lr", 3, 0, 2), ("pa", 3, 0, 1, "g"), ("la", 2, 1, "v"),
+    ("lr", 3, 1, 2), ("iq", 3, 1), ("lr", 3, 1, 0), ("th", 2, 0), ("ln", 3, 0), ("pa", 3, 1, 2, "v"),
+    ("pa", 3, 0, 2, "g"), ("lr", 3, 1, 1), ("ln", 3, 1), ("la", 3, 0, "g"), ("pa", 3, 1, 1, "g"),
+    ("th", 2, 1), ("la", 3, 1, "v"), ("th", 3, 0), ("th", 3, 1),
+)
+
+
+def tile_ryeelman_pa_kernel(
+    tc,
+    invariant_input,
+    equivariant_input,
+    invariant_hidden,
+    equivariant_hidden,
+    W_left,
+    W_right,
+    W_ii,
+    b_ii,
+    out,
+):
+    nc = tc.nc
+    with ExitStack() as ctx:
+        ctx.enter_context(tc.manual_schedule())
+        keep = ctx.enter_context(tc.tile_pool(name="keep", bufs=1))
+        acts = ctx.enter_context(tc.tile_pool(name="acts", bufs=3))
+        work = ctx.enter_context(tc.tile_pool(name="work", bufs=2))
+        wst = ctx.enter_context(tc.tile_pool(name="wst", bufs=2))
+        ep = ctx.enter_context(tc.tile_pool(name="ep", bufs=2))
+        tp = ctx.enter_context(tc.psum_pool(name="tp", bufs=3))
+        mm = ctx.enter_context(tc.psum_pool(name="mm", bufs=5))
+
+        zero_t = keep.tile([P, 1], F32)
+        nc.vector.memset(zero_t[:], 0.0)
+        eps_t = keep.tile([P, 1], F32)
+        nc.vector.tensor_scalar_add(out=eps_t[:], in0=zero_t[:], scalar1=EPS)
+        warm = keep.tile([P, 1], F32)
+        nc.scalar.activation(out=warm[:], in_=eps_t[:], func=ACT.Abs_reciprocal_sqrt)
+        ident = keep.tile([P, P], F32)
+        make_identity(nc, ident[:])
+
+        head_h = keep.tile([P, 24, 16], BF16)
+        head_i = keep.tile([P, 24], BF16)
+        bias_bc = keep.tile([P, 1024], BF16)
+        w_codes = keep.tile([P, 5, 1024], U32, align_bytes=64)
+        w_scales = keep.tile([P, 5, 1024], U8, align_bytes=64)
+        x_codes = keep.tile([P, 3, 1024], U32, align_bytes=64)
+        x_scales = keep.tile([P, 3, 1024], U8, align_bytes=64)
+        i_codes = keep.tile([P, 3, 1024], U32, align_bytes=64)
+        i_scales = keep.tile([P, 3, 1024], U8, align_bytes=64)
+
+        hid_rows = equivariant_hidden.rearrange("(p t) j c -> p (t j) c", t=8)
+        ii_rows = invariant_input.rearrange("(p t) c -> p t c", t=8)
+        ih_rows = invariant_hidden.rearrange("(p t) c -> p t c", t=8)
+        out_rows = out.rearrange("(p t) h -> p t h", t=8)
+        w_src = (W_right, W_left, W_ii[0:512, :], W_ii[512:1024, :], W_ii[1024:1536, :])
+
+        eq_t, inv_t, raw_t, recip, sqs, banks = {}, {}, {}, {}, {}, {}
+
+        def load_eq(bp):
+            eq = acts.tile([P, 6, 512], BF16, tag="eq", bufs=4, align_bytes=64)
+            nc.sync.dma_start(out=eq[:, :, 16:512], in_=hid_rows[:, 6 * bp : 6 * bp + 6, 15:511])
+            eq_t[bp] = eq
+
+        def load_inv(bp):
+            iv = acts.tile([P, 2, 1536], BF16, tag="inv", align_bytes=64)
+            nc.sync.dma_start(out=iv[:, :, 0:512], in_=ii_rows[:, 2 * bp : 2 * bp + 2, :])
+            nc.sync.dma_start(out=iv[:, :, 512:1536], in_=ih_rows[:, 2 * bp : 2 * bp + 2, :])
+            inv_t[bp] = iv
+
+        def load_w(w, hh):
+            raw = wst.tile([P, 4, 512], BF16, tag="raw", bufs=5)
+            for u in range(2):
+                nc.sync.dma_start(
+                    out=raw[:, 2 * u : 2 * u + 2, :],
+                    in_=w_src[w][256 * u : 256 * u + 256, 512 * hh : 512 * hh + 512].rearrange("(p e) c -> p e c", e=2),
+                )
+            raw_t[(w, hh)] = raw
+
+        def heads(bp):
+            nc.vector.tensor_copy(out=eq_t[bp][:, :, 1:16], in_=head_h[:, 6 * bp : 6 * bp + 6, 0:15])
+            nc.vector.tensor_copy(out=eq_t[bp][:, :, 0:1], in_=head_i[:, 6 * bp : 6 * bp + 6].unsqueeze(2))
+
+        def grouped4(ap):
+            return ap.rearrange("p (b u e) -> p b u e", u=2, e=2)
+
+        def eq_group(bp):
+            eq_w = eq_t[bp][:].bitcast(F32)
+            for j in range(3):
+                bank = tp.tile([P, 2, 2, P], F32, tag="tp")
+                for u in range(2):
+                    for t in range(2):
+                        nc.tensor.transpose(bank[:, u, t, :], eq_w[:, 3 * t + j, 128 * u : 128 * u + 128], ident[:])
+                banks[("eq", bp, j)] = bank[:].bitcast(BF16).rearrange("p u t (b e) -> p (t b) u e", e=2)
+
+        def inv_group(bp):
+            inv_w = inv_t[bp][:].bitcast(F32)
+            for g in range(3):
+                bank = tp.tile([P, 2, 2, P], F32, tag="tp")
+                for u in range(2):
+                    for t in range(2):
+                        lo = 256 * g + 128 * u
+                        nc.tensor.transpose(bank[:, u, t, :], inv_w[:, t, lo : lo + 128], ident[:])
+                banks[("inv", bp, g)] = bank[:].rearrange("p u t b -> p (t b) u")
+
+        def square(bp, j):
+            s = work.tile([P, 1024], F32, tag="sq%d" % j)
+            nc.scalar.activation(out=grouped4(s[:]), in_=banks[("eq", bp, j)], func=ACT.Square)
+            sqs[(bp, j)] = s
+
+        def eq_add(bp, j, e):
+            eng = nc.vector if e == "v" else nc.gpsimd
+            eng.tensor_tensor(out=sqs[(bp, 0)][:], in0=sqs[(bp, 0)][:], in1=sqs[(bp, j)][:], op=ALU.add)
+
+        def rsqrt(bp):
+            nc.scalar.activation(
+                out=sqs[(bp, 1)][:], in_=sqs[(bp, 0)][:], func=ACT.Abs_reciprocal_sqrt, bias=eps_t[:]
+            )
+
+        def recip_sq(bp):
+            y = work.tile([P, 1024], F32, tag="y1", bufs=3)
+            nc.scalar.activation(out=y[:], in_=sqs[(bp, 1)][:], func=ACT.Square)
+            recip[bp] = y
+
+        gxs, gis = {}, {}
+
+        def x_mul(bp, j):
+            gx = work.tile([P, 1024], BF16, tag="gx", bufs=3, align_bytes=64)
+            nc.vector.tensor_tensor(
+                out=grouped4(gx[:]), in0=banks[("eq", bp, j)], in1=grouped4(recip[bp][:]), op=ALU.mult
+            )
+            gxs[(bp, j)] = gx
+
+        def x_quant(bp, j):
+            cols = slice(256 * bp, 256 * bp + 256)
+            nc.vector.quantize_mx(
+                out=x_codes[:, j, cols].bitcast(FP8X4), scales=x_scales[:, j, cols], in_=gxs[(bp, j)][:]
+            )
+
+        def i_copy(bp, g, e):
+            gi = work.tile([P, 1024], BF16, tag="gi", bufs=3, align_bytes=64)
+            dst = gi[:].bitcast(F32).rearrange("p (b u) -> p b u", u=2)
+            if e == "s":
+                nc.scalar.copy(out=dst, in_=banks[("inv", bp, g)])
+            else:
+                nc.vector.tensor_copy(out=dst, in_=banks[("inv", bp, g)])
+            gis[(bp, g)] = gi
+
+        def i_quant(bp, g):
+            cols = slice(256 * bp, 256 * bp + 256)
+            nc.vector.quantize_mx(
+                out=i_codes[:, g, cols].bitcast(FP8X4), scales=i_scales[:, g, cols], in_=gis[(bp, g)][:]
+            )
+
+        grps = {}
+
+        def w_regroup(w, hh, e):
+            grp = wst.tile([P, 512, 4], BF16, tag="grp", bufs=2, align_bytes=64)
+            dst = grp[:].rearrange("p (c i) t -> p c t i", i=4)
+            src = raw_t[(w, hh)][:].rearrange("p t (c i) -> p c t i", i=4)
+            if e == "s":
+                nc.scalar.copy(out=dst, in_=src)
+            else:
+                nc.vector.tensor_copy(out=dst, in_=src)
+            grps[(w, hh)] = grp
+
+        def w_quant(w, hh):
+            cols = slice(512 * hh, 512 * hh + 512)
+            nc.vector.quantize_mx(
+                out=w_codes[:, w, cols].bitcast(FP8X4),
+                scales=w_scales[:, w, cols],
+                in_=grps[(w, hh)][:].rearrange("p c t -> p (c t)"),
+            )
+
+        def mx(acc, a_codes, a_scales, row, bs, w, hs, start, stop):
+            nc.tensor.matmul_mx(
+                out=acc[:],
+                lhsT=a_codes[:, row, bs].bitcast(FP8X4),
+                lhsT_scale=a_scales[:, row, bs],
+                rhs=w_codes[:, w, hs].bitcast(FP8X4),
+                rhs_scale=w_scales[:, w, hs],
+                start=start,
+                stop=stop,
+            )
+
+        prods, ys, ress = {}, {}, {}
+
+        def lr_step(bp, hh, j):
+            hs = slice(512 * hh, 512 * hh + 512)
+            p = ep.tile([P, 2, 512], F32, tag="p%d" % j)
+            prods[(bp, hh, j)] = p
+            if (hh, j) == (0, 0):
+                ress[bp] = ep.tile([P, 2, 1024], F32, tag="res", name="res")
+            for t in range(2):
+                bs = slice(256 * bp + 128 * t, 256 * bp + 128 * t + 128)
+                right = mm.tile([P, 512], F32, tag="mm")
+                mx(right, x_codes, x_scales, j, bs, WR, hs, True, True)
+                left = mm.tile([P, 512], F32, tag="mm")
+                mx(left, x_codes, x_scales, j, bs, WL, hs, True, True)
+                rc = ep.tile([P, 512], F32, tag="rc", bufs=3)
+                nc.scalar.copy(out=rc[:], in_=right[:])
+                nc.vector.tensor_tensor(out=p[:, t, :], in0=left[:], in1=rc[:], op=ALU.mult)
+
+        def lin_step(bp, hh):
+            hs = slice(512 * hh, 512 * hh + 512)
+            y = ep.tile([P, 2, 512], F32, tag="y")
+            ys[(bp, hh)] = y
+            for t in range(2):
+                bs = slice(256 * bp + 128 * t, 256 * bp + 128 * t + 128)
+                lin = mm.tile([P, 512], F32, tag="mm")
+                for g in range(3):
+                    mx(lin, i_codes, i_scales, g, bs, WI + g, hs, g == 0, g == 2)
+                nc.vector.tensor_tensor(out=y[:, t, :], in0=lin[:], in1=bias_bc[:, hs], op=ALU.add)
+
+        def p_add(bp, hh, j, e):
+            eng = nc.vector if e == "v" else nc.gpsimd
+            eng.tensor_tensor(out=prods[(bp, hh, 0)][:], in0=prods[(bp, hh, 0)][:], in1=prods[(bp, hh, j)][:], op=ALU.add)
+
+        def last_add(bp, hh, e):
+            hs = slice(512 * hh, 512 * hh + 512)
+            eng = nc.vector if e == "v" else nc.gpsimd
+            eng.tensor_tensor(out=ress[bp][:, :, hs], in0=prods[(bp, hh, 0)][:], in1=ys[(bp, hh)][:], op=ALU.add)
+
+        def tanh_store(bp, t):
+            nc.scalar.activation(out=ress[bp][:, t, :], in_=ress[bp][:, t, :], func=ACT.Tanh)
+            nc.sync.dma_start(out=out_rows[:, 2 * bp + t, :], in_=ress[bp][:, t, :])
+
+        with nc.allow_non_contiguous_dma(reason="the first 16 channels arrive in short runs"):
+            nc.scalar.dma_start(out=head_i[:], in_=equivariant_input.rearrange("(p t) j -> p (t j)", t=8))
+            nc.scalar.dma_start(out=head_h[:, 0:6, 0:15], in_=hid_rows[:, 0:6, 0:15])
+            nc.scalar.dma_start(out=head_h[:, 6:24, 0:15], in_=hid_rows[:, 6:24, 0:15])
+        nc.gpsimd.dma_start(out=bias_bc[:], in_=b_ii.partition_broadcast(P))
+        todo = {
+            "le": load_eq, "li": load_inv, "lw": load_w, "hd": heads, "e1": eq_group, "e2": eq_group, "it": inv_group,
+            "sq": square, "ea": eq_add, "rs": rsqrt, "sy": recip_sq, "xm": x_mul, "xq": x_quant,
+            "ic": i_copy, "iq": i_quant, "wr": w_regroup, "wq": w_quant, "lr": lr_step, "ln": lin_step,
+            "pa": p_add, "la": last_add, "th": tanh_store,
+        }
+        for piece in ORDER:
+            todo[piece[0]](*piece[1:])

@@ -15,39 +15,7 @@ FLOPS = 2 * (2 * 3072 * 512 * 1024 + 1024 * 1536 * 1024)
 EPS = 1e-6
 P = 128
 WR, WL, WI = 0, 1, 2
-ORDER = (
-    ("le", 0), ("hd", 0), ("lw", 1, 0), ("le", 1), ("le", 2), ("e1", 0), ("lw", 0, 0), ("hd", 1),
-    ("sq", 0, 0), ("sq", 0, 2), ("sq", 0, 1), ("e1", 1), ("wr", 1, 0, "v"), ("lw", 2, 0), ("hd", 2),
-    ("ea", 0, 2, "g"), ("ea", 0, 1, "v"), ("lw", 4, 0), ("wr", 0, 0, "v"), ("wq", 0, 0), ("lw", 3, 0),
-    ("sq", 1, 0), ("rs", 0), ("sy", 0), ("li", 0), ("sq", 1, 1), ("wq", 1, 0), ("sq", 1, 2),
-    ("wr", 2, 0, "s"), ("e2", 0), ("xm", 0, 0), ("xm", 0, 1), ("lw", 2, 1), ("xm", 0, 2), ("xq", 0, 1),
-    ("xq", 0, 0), ("ea", 1, 1, "g"), ("le", 3), ("ea", 1, 2, "g"), ("lw", 1, 1), ("xq", 0, 2), ("it", 0),
-    ("wq", 2, 0), ("li", 1), ("ic", 0, 2, "s"), ("iq", 0, 2), ("lr", 0, 0, 0), ("ic", 0, 0, "s"), ("li", 2),
-    ("ic", 0, 1, "v"), ("rs", 1), ("sy", 1), ("wr", 3, 0, "v"), ("e1", 2), ("sq", 2, 0), ("iq", 0, 1),
-    ("wr", 4, 0, "v"), ("wq", 3, 0), ("lr", 0, 0, 1), ("sq", 2, 2), ("wq", 4, 0), ("lw", 0, 1), ("iq", 0, 0),
-    ("sq", 2, 1), ("lw", 3, 1), ("wr", 0, 1, "v"), ("lr", 0, 0, 2), ("hd", 3), ("wr", 1, 1, "s"), ("it", 1),
-    ("ic", 1, 1, "s"), ("wq", 0, 1), ("pa", 0, 0, 1, "g"), ("ln", 0, 0), ("ic", 1, 0, "s"), ("wq", 1, 1),
-    ("pa", 0, 0, 2, "g"), ("wr", 2, 1, "v"), ("lr", 0, 1, 2), ("iq", 1, 0), ("wq", 2, 1), ("ic", 1, 2, "s"),
-    ("li", 3), ("lw", 4, 1), ("ea", 2, 2, "g"), ("lr", 0, 1, 0), ("e2", 1), ("wr", 4, 1, "s"),
-    ("la", 0, 0, "g"), ("iq", 1, 2), ("xm", 1, 0), ("xm", 1, 1), ("iq", 1, 1), ("xq", 1, 0),
-    ("wr", 3, 1, "s"), ("wq", 3, 1), ("ea", 2, 1, "g"), ("pa", 0, 1, 2, "g"), ("wq", 4, 1), ("lr", 0, 1, 1),
-    ("xq", 1, 1), ("rs", 2), ("sy", 2), ("ln", 0, 1), ("lr", 1, 0, 1), ("xm", 1, 2), ("pa", 0, 1, 1, "g"),
-    ("xq", 1, 2), ("lr", 1, 0, 0), ("e1", 3), ("sq", 3, 0), ("pa", 1, 0, 1, "v"), ("sq", 3, 1),
-    ("la", 0, 1, "g"), ("lr", 1, 0, 2), ("sq", 3, 2), ("ea", 3, 1, "v"), ("ea", 3, 2, "g"), ("lr", 1, 1, 0),
-    ("it", 2), ("ic", 2, 1, "s"), ("pa", 1, 0, 2, "g"), ("ln", 1, 0), ("ic", 2, 2, "s"), ("ic", 2, 0, "s"),
-    ("iq", 2, 0), ("rs", 3), ("iq", 2, 2), ("e2", 2), ("xm", 2, 0), ("xq", 2, 0), ("iq", 2, 1),
-    ("lr", 1, 1, 1), ("lr", 1, 1, 2), ("xm", 2, 2), ("la", 1, 0, "g"), ("xm", 2, 1), ("th", 0, 1),
-    ("pa", 1, 1, 2, "g"), ("ln", 2, 0), ("ln", 1, 1), ("xq", 2, 1), ("pa", 1, 1, 1, "g"), ("it", 3),
-    ("th", 0, 0), ("la", 1, 1, "g"), ("xq", 2, 2), ("lr", 2, 0, 0), ("lr", 2, 0, 2), ("lr", 2, 0, 1),
-    ("lr", 2, 1, 0), ("ic", 3, 2, "v"), ("ic", 3, 0, "s"), ("sy", 3), ("pa", 2, 0, 2, "g"),
-    ("ic", 3, 1, "s"), ("e2", 3), ("iq", 3, 2), ("th", 1, 1), ("pa", 2, 0, 1, "g"), ("iq", 3, 0),
-    ("xm", 3, 0), ("xq", 3, 0), ("xm", 3, 1), ("th", 1, 0), ("la", 2, 0, "g"), ("xm", 3, 2), ("lr", 2, 1, 2),
-    ("pa", 2, 1, 2, "g"), ("lr", 2, 1, 1), ("xq", 3, 1), ("pa", 2, 1, 1, "g"), ("ln", 2, 1), ("xq", 3, 2),
-    ("lr", 3, 0, 0), ("lr", 3, 0, 1), ("lr", 3, 0, 2), ("pa", 3, 0, 1, "g"), ("la", 2, 1, "v"),
-    ("lr", 3, 1, 2), ("iq", 3, 1), ("lr", 3, 1, 0), ("th", 2, 0), ("ln", 3, 0), ("pa", 3, 1, 2, "v"),
-    ("pa", 3, 0, 2, "g"), ("lr", 3, 1, 1), ("ln", 3, 1), ("la", 3, 0, "g"), ("pa", 3, 1, 1, "g"),
-    ("th", 2, 1), ("la", 3, 1, "v"), ("th", 3, 0), ("th", 3, 1),
-)
+PE_ADDS = 4
 
 
 def tile_ryeelman_pa_kernel(
@@ -69,9 +37,10 @@ def tile_ryeelman_pa_kernel(
         acts = ctx.enter_context(tc.tile_pool(name="acts", bufs=3))
         work = ctx.enter_context(tc.tile_pool(name="work", bufs=2))
         wst = ctx.enter_context(tc.tile_pool(name="wst", bufs=2))
-        ep = ctx.enter_context(tc.tile_pool(name="ep", bufs=2))
+        ep = ctx.enter_context(tc.tile_pool(name="ep", bufs=3))
         tp = ctx.enter_context(tc.psum_pool(name="tp", bufs=3))
-        mm = ctx.enter_context(tc.psum_pool(name="mm", bufs=5))
+        mm = ctx.enter_context(tc.psum_pool(name="mm", bufs=4))
+        ob = ctx.enter_context(tc.psum_pool(name="ob", bufs=1))
 
         zero_t = keep.tile([P, 1], F32)
         nc.vector.memset(zero_t[:], 0.0)
@@ -81,10 +50,13 @@ def tile_ryeelman_pa_kernel(
         nc.scalar.activation(out=warm[:], in_=eps_t[:], func=ACT.Abs_reciprocal_sqrt)
         ident = keep.tile([P, P], F32)
         make_identity(nc, ident[:])
+        ident_b = keep.tile([P, P], BF16)
+        make_identity(nc, ident_b[:])
 
         head_h = keep.tile([P, 24, 16], BF16)
         head_i = keep.tile([P, 24], BF16)
-        bias_bc = keep.tile([P, 1024], BF16)
+        bias_rows = keep.tile([P, P], BF16)
+        bias_t = keep.tile([P, 8], F32)
         w_codes = keep.tile([P, 5, 1024], U32, align_bytes=64)
         w_scales = keep.tile([P, 5, 1024], U8, align_bytes=64)
         x_codes = keep.tile([P, 3, 1024], U32, align_bytes=64)
@@ -98,7 +70,7 @@ def tile_ryeelman_pa_kernel(
         out_rows = out.rearrange("(p t) h -> p t h", t=8)
         w_src = (W_right, W_left, W_ii[0:512, :], W_ii[512:1024, :], W_ii[1024:1536, :])
 
-        eq_t, inv_t, raw_t, recip, sqs, banks = {}, {}, {}, {}, {}, {}
+        eq_t, inv_t, raw_t, grp_t, recip, sqs, banks, gxs, gis, prods, outs = {}, {}, {}, {}, {}, {}, {}, {}, {}, {}, {}
 
         def load_eq(bp):
             eq = acts.tile([P, 6, 512], BF16, tag="eq", bufs=4, align_bytes=64)
@@ -127,45 +99,38 @@ def tile_ryeelman_pa_kernel(
         def grouped4(ap):
             return ap.rearrange("p (b u e) -> p b u e", u=2, e=2)
 
-        def eq_group(bp):
+        def eq_bank(bp, j, pool=tp, tag="tp"):
             eq_w = eq_t[bp][:].bitcast(F32)
-            for j in range(3):
-                bank = tp.tile([P, 2, 2, P], F32, tag="tp")
-                for u in range(2):
-                    for t in range(2):
-                        nc.tensor.transpose(bank[:, u, t, :], eq_w[:, 3 * t + j, 128 * u : 128 * u + 128], ident[:])
-                banks[("eq", bp, j)] = bank[:].bitcast(BF16).rearrange("p u t (b e) -> p (t b) u e", e=2)
+            bank = pool.tile([P, 2, 2, P], F32, tag=tag)
+            for u in range(2):
+                for t in range(2):
+                    nc.tensor.transpose(bank[:, u, t, :], eq_w[:, 3 * t + j, 128 * u : 128 * u + 128], ident[:])
+            banks[("eq", bp, j)] = bank[:].bitcast(BF16).rearrange("p u t (b e) -> p (t b) u e", e=2)
 
-        def inv_group(bp):
+        def inv_bank(bp, g):
             inv_w = inv_t[bp][:].bitcast(F32)
-            for g in range(3):
-                bank = tp.tile([P, 2, 2, P], F32, tag="tp")
-                for u in range(2):
-                    for t in range(2):
-                        lo = 256 * g + 128 * u
-                        nc.tensor.transpose(bank[:, u, t, :], inv_w[:, t, lo : lo + 128], ident[:])
-                banks[("inv", bp, g)] = bank[:].rearrange("p u t b -> p (t b) u")
+            bank = tp.tile([P, 2, 2, P], F32, tag="tp")
+            for u in range(2):
+                for t in range(2):
+                    lo = 256 * g + 128 * u
+                    nc.tensor.transpose(bank[:, u, t, :], inv_w[:, t, lo : lo + 128], ident[:])
+            banks[("inv", bp, g)] = bank[:].rearrange("p u t b -> p (t b) u")
 
         def square(bp, j):
             s = work.tile([P, 1024], F32, tag="sq%d" % j)
             nc.scalar.activation(out=grouped4(s[:]), in_=banks[("eq", bp, j)], func=ACT.Square)
             sqs[(bp, j)] = s
 
-        def eq_add(bp, j, e):
-            eng = nc.vector if e == "v" else nc.gpsimd
+        def eq_add(eng, bp, j):
             eng.tensor_tensor(out=sqs[(bp, 0)][:], in0=sqs[(bp, 0)][:], in1=sqs[(bp, j)][:], op=ALU.add)
 
-        def rsqrt(bp):
+        def reciprocal(bp):
             nc.scalar.activation(
                 out=sqs[(bp, 1)][:], in_=sqs[(bp, 0)][:], func=ACT.Abs_reciprocal_sqrt, bias=eps_t[:]
             )
-
-        def recip_sq(bp):
             y = work.tile([P, 1024], F32, tag="y1", bufs=3)
             nc.scalar.activation(out=y[:], in_=sqs[(bp, 1)][:], func=ACT.Square)
             recip[bp] = y
-
-        gxs, gis = {}, {}
 
         def x_mul(bp, j):
             gx = work.tile([P, 1024], BF16, tag="gx", bufs=3, align_bytes=64)
@@ -180,13 +145,9 @@ def tile_ryeelman_pa_kernel(
                 out=x_codes[:, j, cols].bitcast(FP8X4), scales=x_scales[:, j, cols], in_=gxs[(bp, j)][:]
             )
 
-        def i_copy(bp, g, e):
+        def i_copy(bp, g):
             gi = work.tile([P, 1024], BF16, tag="gi", bufs=3, align_bytes=64)
-            dst = gi[:].bitcast(F32).rearrange("p (b u) -> p b u", u=2)
-            if e == "s":
-                nc.scalar.copy(out=dst, in_=banks[("inv", bp, g)])
-            else:
-                nc.vector.tensor_copy(out=dst, in_=banks[("inv", bp, g)])
+            nc.scalar.copy(out=gi[:].bitcast(F32).rearrange("p (b u) -> p b u", u=2), in_=banks[("inv", bp, g)])
             gis[(bp, g)] = gi
 
         def i_quant(bp, g):
@@ -195,89 +156,216 @@ def tile_ryeelman_pa_kernel(
                 out=i_codes[:, g, cols].bitcast(FP8X4), scales=i_scales[:, g, cols], in_=gis[(bp, g)][:]
             )
 
-        grps = {}
-
-        def w_regroup(w, hh, e):
-            grp = wst.tile([P, 512, 4], BF16, tag="grp", bufs=2, align_bytes=64)
+        def w_regroup(w, hh):
+            on_scalar = (w, hh) == (WI + 2, 0)
+            grp = wst.tile([P, 512, 4], BF16, tag=("grs" if on_scalar else "grp"), bufs=(1 if on_scalar else 2), align_bytes=64)
             dst = grp[:].rearrange("p (c i) t -> p c t i", i=4)
             src = raw_t[(w, hh)][:].rearrange("p t (c i) -> p c t i", i=4)
-            if e == "s":
+            if on_scalar:
                 nc.scalar.copy(out=dst, in_=src)
             else:
                 nc.vector.tensor_copy(out=dst, in_=src)
-            grps[(w, hh)] = grp
+            grp_t[(w, hh)] = grp
 
         def w_quant(w, hh):
             cols = slice(512 * hh, 512 * hh + 512)
             nc.vector.quantize_mx(
                 out=w_codes[:, w, cols].bitcast(FP8X4),
                 scales=w_scales[:, w, cols],
-                in_=grps[(w, hh)][:].rearrange("p c t -> p (c t)"),
+                in_=grp_t[(w, hh)][:].rearrange("p c t -> p (c t)"),
             )
 
-        def mx(acc, a_codes, a_scales, row, bs, w, hs, start, stop):
+        def mx(acc, w, hp, hl, a_codes, a_scales, row, bp, start, stop):
+            hcols = slice(256 * hp + 128 * hl, 256 * hp + 128 * hl + 128)
+            bcols = slice(256 * bp, 256 * bp + 256)
             nc.tensor.matmul_mx(
-                out=acc[:],
-                lhsT=a_codes[:, row, bs].bitcast(FP8X4),
-                lhsT_scale=a_scales[:, row, bs],
-                rhs=w_codes[:, w, hs].bitcast(FP8X4),
-                rhs_scale=w_scales[:, w, hs],
+                out=acc,
+                lhsT=w_codes[:, w, hcols].bitcast(FP8X4),
+                lhsT_scale=w_scales[:, w, hcols],
+                rhs=a_codes[:, row, bcols].bitcast(FP8X4),
+                rhs_scale=a_scales[:, row, bcols],
                 start=start,
                 stop=stop,
             )
 
-        prods, ys, ress = {}, {}, {}
-
-        def lr_step(bp, hh, j):
-            hs = slice(512 * hh, 512 * hh + 512)
-            p = ep.tile([P, 2, 512], F32, tag="p%d" % j)
-            prods[(bp, hh, j)] = p
-            if (hh, j) == (0, 0):
-                ress[bp] = ep.tile([P, 2, 1024], F32, tag="res", name="res")
-            for t in range(2):
-                bs = slice(256 * bp + 128 * t, 256 * bp + 128 * t + 128)
-                right = mm.tile([P, 512], F32, tag="mm")
-                mx(right, x_codes, x_scales, j, bs, WR, hs, True, True)
-                left = mm.tile([P, 512], F32, tag="mm")
-                mx(left, x_codes, x_scales, j, bs, WL, hs, True, True)
-                rc = ep.tile([P, 512], F32, tag="rc", bufs=3)
+        def products(u):
+            bp, hp = u // 4, u % 4
+            for j in range(3):
+                right = mm.tile([P, 2, 256], F32, tag="mm")
+                for hl in range(2):
+                    mx(right[:, hl, :], WR, hp, hl, x_codes, x_scales, j, bp, True, True)
+                left = mm.tile([P, 2, 256], F32, tag="mm")
+                for hl in range(2):
+                    mx(left[:, hl, :], WL, hp, hl, x_codes, x_scales, j, bp, True, True)
+                rc = ep.tile([P, 2, 256], F32, tag="rc")
                 nc.scalar.copy(out=rc[:], in_=right[:])
-                nc.vector.tensor_tensor(out=p[:, t, :], in0=left[:], in1=rc[:], op=ALU.mult)
+                p = ep.tile([P, 2, 256], F32, tag="p%d" % j, bufs=6)
+                nc.vector.tensor_tensor(out=p[:], in0=left[:], in1=rc[:], op=ALU.mult)
+                prods[(u, j)] = p
 
-        def lin_step(bp, hh):
-            hs = slice(512 * hh, 512 * hh + 512)
-            y = ep.tile([P, 2, 512], F32, tag="y")
-            ys[(bp, hh)] = y
-            for t in range(2):
-                bs = slice(256 * bp + 128 * t, 256 * bp + 128 * t + 128)
-                lin = mm.tile([P, 512], F32, tag="mm")
+        def linear(u):
+            bp, hp = u // 4, u % 4
+            lin = mm.tile([P, 2, 256], F32, tag="mm")
+            for hl in range(2):
                 for g in range(3):
-                    mx(lin, i_codes, i_scales, g, bs, WI + g, hs, g == 0, g == 2)
-                nc.vector.tensor_tensor(out=y[:, t, :], in0=lin[:], in1=bias_bc[:, hs], op=ALU.add)
+                    mx(lin[:, hl, :], WI + g, hp, hl, i_codes, i_scales, g, bp, g == 0, g == 2)
+            for hl in range(2):
+                nc.vector.scalar_tensor_tensor(
+                    out=prods[(u, 0)][:, hl, :],
+                    in0=lin[:, hl, :],
+                    scalar=bias_t[:, 2 * hp + hl : 2 * hp + hl + 1],
+                    in1=prods[(u, 0)][:, hl, :],
+                    op0=ALU.add,
+                    op1=ALU.add,
+                )
 
-        def p_add(bp, hh, j, e):
-            eng = nc.vector if e == "v" else nc.gpsimd
-            eng.tensor_tensor(out=prods[(bp, hh, 0)][:], in0=prods[(bp, hh, 0)][:], in1=prods[(bp, hh, j)][:], op=ALU.add)
+        def pair_add(u):
+            if u >= PE_ADDS:
+                nc.gpsimd.tensor_tensor(out=prods[(u, 1)][:], in0=prods[(u, 1)][:], in1=prods[(u, 2)][:], op=ALU.add)
 
-        def last_add(bp, hh, e):
-            hs = slice(512 * hh, 512 * hh + 512)
-            eng = nc.vector if e == "v" else nc.gpsimd
-            eng.tensor_tensor(out=ress[bp][:, :, hs], in0=prods[(bp, hh, 0)][:], in1=ys[(bp, hh)][:], op=ALU.add)
+        def last_add(u):
+            if u >= PE_ADDS:
+                nc.gpsimd.tensor_tensor(out=prods[(u, 0)][:], in0=prods[(u, 0)][:], in1=prods[(u, 1)][:], op=ALU.add)
 
-        def tanh_store(bp, t):
-            nc.scalar.activation(out=ress[bp][:, t, :], in_=ress[bp][:, t, :], func=ACT.Tanh)
-            nc.sync.dma_start(out=out_rows[:, 2 * bp + t, :], in_=ress[bp][:, t, :])
+        def turn_back(u):
+            o = ob.tile([P, 2, 2, P], F32, tag="ob")
+            terms = 3 if u < PE_ADDS else 1
+            for t in range(2):
+                for hl in range(2):
+                    for i in range(terms):
+                        nc.tensor.matmul(
+                            out=o[:, t, hl, :],
+                            lhsT=prods[(u, i)][:, hl, 128 * t : 128 * t + 128],
+                            rhs=ident[:],
+                            is_transpose=True,
+                            start=(i == 0),
+                            stop=(i == terms - 1),
+                        )
+            outs[u] = o
+
+        def finish(u):
+            bp, hp = u // 4, u % 4
+            res = ep.tile([P, 2, 256], F32, tag="res")
+            nc.scalar.activation(out=res[:], in_=outs[u][:].rearrange("p t l h -> p t (l h)"), func=ACT.Tanh)
+            nc.sync.dma_start(out=out_rows[:, 2 * bp : 2 * bp + 2, 256 * hp : 256 * hp + 256], in_=res[:])
 
         with nc.allow_non_contiguous_dma(reason="the first 16 channels arrive in short runs"):
             nc.scalar.dma_start(out=head_i[:], in_=equivariant_input.rearrange("(p t) j -> p (t j)", t=8))
             nc.scalar.dma_start(out=head_h[:, 0:6, 0:15], in_=hid_rows[:, 0:6, 0:15])
             nc.scalar.dma_start(out=head_h[:, 6:24, 0:15], in_=hid_rows[:, 6:24, 0:15])
-        nc.gpsimd.dma_start(out=bias_bc[:], in_=b_ii.partition_broadcast(P))
-        todo = {
-            "le": load_eq, "li": load_inv, "lw": load_w, "hd": heads, "e1": eq_group, "e2": eq_group, "it": inv_group,
-            "sq": square, "ea": eq_add, "rs": rsqrt, "sy": recip_sq, "xm": x_mul, "xq": x_quant,
-            "ic": i_copy, "iq": i_quant, "wr": w_regroup, "wq": w_quant, "lr": lr_step, "ln": lin_step,
-            "pa": p_add, "la": last_add, "th": tanh_store,
-        }
-        for piece in ORDER:
-            todo[piece[0]](*piece[1:])
+        nc.vector.memset(bias_rows[:], 0.0)
+        nc.gpsimd.dma_start(out=bias_rows[0:8, :], in_=b_ii.rearrange("(r c) -> r c", c=P))
+        load_eq(0)
+        load_w(WR, 0)
+        load_w(WL, 0)
+        load_eq(1)
+        load_w(WI, 0)
+        load_inv(0)
+        load_w(WI + 1, 0)
+        load_w(WI + 2, 0)
+        load_eq(2)
+        load_eq(3)
+        load_inv(1)
+
+        heads(0)
+        heads(1)
+        for j in range(3):
+            eq_bank(0, j)
+        w_regroup(WR, 0)
+        for j in range(3):
+            square(0, j)
+            if j:
+                eq_add(nc.vector, 0, j)
+        reciprocal(0)
+        w_regroup(WL, 0)
+        for w in (WR, WL):
+            w_quant(w, 0)
+            load_w(w, 1)
+        bias_ps = ob.tile([P, P], BF16, tag="ob")
+        nc.tensor.transpose(bias_ps[:], bias_rows[:], ident_b[:])
+        nc.vector.tensor_copy(out=bias_t[:], in_=bias_ps[:, 0:8])
+        heads(2)
+        heads(3)
+        for j in range(3):
+            eq_bank(0, j)
+        for j in range(3):
+            eq_bank(1, j, mm, "mm")
+        for j in range(3):
+            x_mul(0, j)
+            if j:
+                x_quant(0, j - 1)
+            square(1, j)
+            if j:
+                eq_add(nc.gpsimd, 1, j)
+        x_quant(0, 2)
+
+        def banks_for(u):
+            bp, hp = u // 4, u % 4
+            if hp == 0 and bp < 4:
+                for g in range(3):
+                    inv_bank(bp, g)
+            if u in (1, 2):
+                for j in range(3):
+                    eq_bank(u + 1, j)
+            if u == 3:
+                for j in range(3):
+                    eq_bank(1, j)
+            if 1 <= bp < 3 and hp:
+                eq_bank(bp + 1, hp - 1)
+
+        def side(u):
+            bp, hp = u // 4, u % 4
+            if hp == 0 and bp < 4:
+                for g in range(3):
+                    i_copy(bp, g)
+            if u < 3:
+                hh = 0 if u == 0 else 1
+                for w in ((WI, WI + 1, WI + 2), (WR, WL), (WI, WI + 1, WI + 2))[u]:
+                    w_regroup(w, hh)
+                    w_quant(w, hh)
+                    if hh == 0:
+                        load_w(w, 1)
+            if u == 0:
+                load_inv(2)
+                load_inv(3)
+                reciprocal(1)
+            if hp == 0 and bp < 4:
+                for g in range(3):
+                    i_quant(bp, g)
+            if u in (1, 2):
+                for j in range(3):
+                    square(u + 1, j)
+                    if j:
+                        eq_add(nc.gpsimd, u + 1, j)
+            if u in (2, 3):
+                reciprocal(u)
+            if u == 3:
+                for j in range(3):
+                    x_mul(1, j)
+                    if j:
+                        x_quant(1, j - 1)
+                x_quant(1, 2)
+            if 1 <= bp < 3 and hp:
+                x_mul(bp + 1, hp - 1)
+                if hp > 1:
+                    x_quant(bp + 1, hp - 2)
+                if hp == 3:
+                    x_quant(bp + 1, 2)
+
+        banks_for(0)
+        for u in range(18):
+            if u < 16:
+                products(u)
+                pair_add(u)
+            if 1 <= u < 17:
+                linear(u - 1)
+                last_add(u - 1)
+            side(u)
+            done = [v for v in range(16) if max(v + 2, 3 + v // 2) == u]
+            for v in done:
+                turn_back(v)
+                if v != done[-1]:
+                    finish(v)
+            banks_for(u + 1)
+            if done:
+                finish(done[-1])

@@ -39,8 +39,7 @@ def tile_ryeelman_pa_kernel(
         wst = ctx.enter_context(tc.tile_pool(name="wst", bufs=2))
         ep = ctx.enter_context(tc.tile_pool(name="ep", bufs=3))
         tp = ctx.enter_context(tc.psum_pool(name="tp", bufs=3))
-        mm = ctx.enter_context(tc.psum_pool(name="mm", bufs=4))
-        ob = ctx.enter_context(tc.psum_pool(name="ob", bufs=1))
+        mm = ctx.enter_context(tc.psum_pool(name="mm", bufs=5))
 
         zero_t = keep.tile([P, 1], F32)
         nc.vector.memset(zero_t[:], 0.0)
@@ -190,15 +189,19 @@ def tile_ryeelman_pa_kernel(
 
         def products(u):
             bp, hp = u // 4, u % 4
+            rcs = []
             for j in range(3):
                 right = mm.tile([P, 2, 256], F32, tag="mm")
                 for hl in range(2):
                     mx(right[:, hl, :], WR, hp, hl, x_codes, x_scales, j, bp, True, True)
+                rc = ep.tile([P, 2, 256], F32, tag="rc", bufs=4)
+                nc.scalar.copy(out=rc[:], in_=right[:])
+                rcs.append(rc)
+            for j in range(3):
+                rc = rcs[j]
                 left = mm.tile([P, 2, 256], F32, tag="mm")
                 for hl in range(2):
                     mx(left[:, hl, :], WL, hp, hl, x_codes, x_scales, j, bp, True, True)
-                rc = ep.tile([P, 2, 256], F32, tag="rc")
-                nc.scalar.copy(out=rc[:], in_=right[:])
                 p = ep.tile([P, 2, 256], F32, tag="p%d" % j, bufs=6)
                 nc.vector.tensor_tensor(out=p[:], in0=left[:], in1=rc[:], op=ALU.mult)
                 prods[(u, j)] = p
@@ -228,7 +231,7 @@ def tile_ryeelman_pa_kernel(
                 nc.gpsimd.tensor_tensor(out=prods[(u, 0)][:], in0=prods[(u, 0)][:], in1=prods[(u, 1)][:], op=ALU.add)
 
         def turn_back(u):
-            o = ob.tile([P, 2, 2, P], F32, tag="ob")
+            o = mm.tile([P, 2, 2, P], F32, tag="mm")
             terms = 3 if u < PE_ADDS else 1
             for t in range(2):
                 for hl in range(2):
@@ -268,20 +271,20 @@ def tile_ryeelman_pa_kernel(
         load_inv(1)
 
         heads(0)
-        heads(1)
         for j in range(3):
             eq_bank(0, j)
         w_regroup(WR, 0)
+        w_regroup(WL, 0)
         for j in range(3):
             square(0, j)
             if j:
                 eq_add(nc.vector, 0, j)
         reciprocal(0)
-        w_regroup(WL, 0)
         for w in (WR, WL):
             w_quant(w, 0)
             load_w(w, 1)
-        bias_ps = ob.tile([P, P], BF16, tag="ob")
+        heads(1)
+        bias_ps = mm.tile([P, P], BF16, tag="mm")
         nc.tensor.transpose(bias_ps[:], bias_rows[:], ident_b[:])
         nc.vector.tensor_copy(out=bias_t[:], in_=bias_ps[:, 0:8])
         heads(2)
@@ -292,12 +295,10 @@ def tile_ryeelman_pa_kernel(
             eq_bank(1, j, mm, "mm")
         for j in range(3):
             x_mul(0, j)
-            if j:
-                x_quant(0, j - 1)
+            x_quant(0, j)
             square(1, j)
-            if j:
-                eq_add(nc.gpsimd, 1, j)
-        x_quant(0, 2)
+        for j in (1, 2):
+            eq_add(nc.vector, 1, j)
 
         def banks_for(u):
             bp, hp = u // 4, u % 4
@@ -345,18 +346,20 @@ def tile_ryeelman_pa_kernel(
                     if j:
                         x_quant(1, j - 1)
                 x_quant(1, 2)
+
+        def early(u):
+            bp, hp = u // 4, u % 4
             if 1 <= bp < 3 and hp:
                 x_mul(bp + 1, hp - 1)
-                if hp > 1:
-                    x_quant(bp + 1, hp - 2)
-                if hp == 3:
-                    x_quant(bp + 1, 2)
+                x_quant(bp + 1, hp - 1)
 
-        banks_for(0)
         for u in range(18):
+            early(u)
             if u < 16:
                 products(u)
                 pair_add(u)
+            if u == 0:
+                banks_for(0)
             if 1 <= u < 17:
                 linear(u - 1)
                 last_add(u - 1)

@@ -14,8 +14,9 @@ ALU = mybir.AluOpType
 FLOPS = 2 * (2 * 3072 * 512 * 1024 + 1024 * 1536 * 1024)
 EPS = 1e-6
 P = 128
-WR, WL, WI = 0, 1, 2
-PE_ADDS = 4
+GROUPS = 4
+ROUNDS = 16
+W_R, W_L, W_I = 0, 1, 2
 
 
 def tile_ryeelman_pa_kernel(
@@ -36,26 +37,26 @@ def tile_ryeelman_pa_kernel(
         keep = ctx.enter_context(tc.tile_pool(name="keep", bufs=1))
         acts = ctx.enter_context(tc.tile_pool(name="acts", bufs=3))
         work = ctx.enter_context(tc.tile_pool(name="work", bufs=2))
-        wst = ctx.enter_context(tc.tile_pool(name="wst", bufs=2))
-        ep = ctx.enter_context(tc.tile_pool(name="ep", bufs=3))
-        tp = ctx.enter_context(tc.psum_pool(name="tp", bufs=3))
-        mm = ctx.enter_context(tc.psum_pool(name="mm", bufs=5))
+        stage = ctx.enter_context(tc.tile_pool(name="stage", bufs=2))
+        block = ctx.enter_context(tc.tile_pool(name="block", bufs=3))
+        ahead = ctx.enter_context(tc.psum_pool(name="ahead", bufs=3))
+        ring = ctx.enter_context(tc.psum_pool(name="ring", bufs=5))
 
-        zero_t = keep.tile([P, 1], F32)
-        nc.vector.memset(zero_t[:], 0.0)
-        eps_t = keep.tile([P, 1], F32)
-        nc.vector.tensor_scalar_add(out=eps_t[:], in0=zero_t[:], scalar1=EPS)
+        zero = keep.tile([P, 1], F32)
+        nc.vector.memset(zero[:], 0.0)
+        eps = keep.tile([P, 1], F32)
+        nc.vector.tensor_scalar_add(out=eps[:], in0=zero[:], scalar1=EPS)
         warm = keep.tile([P, 1], F32)
-        nc.scalar.activation(out=warm[:], in_=eps_t[:], func=ACT.Abs_reciprocal_sqrt)
+        nc.scalar.activation(out=warm[:], in_=eps[:], func=ACT.Abs_reciprocal_sqrt)
         ident = keep.tile([P, P], F32)
         make_identity(nc, ident[:])
-        ident_b = keep.tile([P, P], BF16)
-        make_identity(nc, ident_b[:])
+        ident_bf = keep.tile([P, P], BF16)
+        make_identity(nc, ident_bf[:])
 
-        head_h = keep.tile([P, 24, 16], BF16)
-        head_i = keep.tile([P, 24], BF16)
+        head_hidden = keep.tile([P, 24, 16], BF16)
+        head_input = keep.tile([P, 24], BF16)
         bias_rows = keep.tile([P, P], BF16)
-        bias_t = keep.tile([P, 8], F32)
+        bias = keep.tile([P, 8], F32)
         w_codes = keep.tile([P, 5, 1024], U32, align_bytes=64)
         w_scales = keep.tile([P, 5, 1024], U8, align_bytes=64)
         x_codes = keep.tile([P, 3, 1024], U32, align_bytes=64)
@@ -63,209 +64,199 @@ def tile_ryeelman_pa_kernel(
         i_codes = keep.tile([P, 3, 1024], U32, align_bytes=64)
         i_scales = keep.tile([P, 3, 1024], U8, align_bytes=64)
 
-        hid_rows = equivariant_hidden.rearrange("(p t) j c -> p (t j) c", t=8)
-        ii_rows = invariant_input.rearrange("(p t) c -> p t c", t=8)
-        ih_rows = invariant_hidden.rearrange("(p t) c -> p t c", t=8)
-        out_rows = out.rearrange("(p t) h -> p t h", t=8)
-        w_src = (W_right, W_left, W_ii[0:512, :], W_ii[512:1024, :], W_ii[1024:1536, :])
+        hidden_rows = equivariant_hidden.rearrange("(p s) j c -> p (s j) c", s=8)
+        input_rows = invariant_input.rearrange("(p s) c -> p s c", s=8)
+        state_rows = invariant_hidden.rearrange("(p s) c -> p s c", s=8)
+        out_rows = out.rearrange("(p s) h -> p s h", s=8)
+        w_hbm = (W_right, W_left, W_ii[0:512, :], W_ii[512:1024, :], W_ii[1024:1536, :])
 
-        eq_t, inv_t, raw_t, grp_t, recip, sqs, banks, gxs, gis, prods, outs = {}, {}, {}, {}, {}, {}, {}, {}, {}, {}, {}
+        eq_sb, inv_sb, w_raw, w_grouped = {}, {}, {}, {}
+        banks, squares, recip, x_grouped, i_grouped, terms, turned = {}, {}, {}, {}, {}, {}, {}
 
-        def load_eq(bp):
-            eq = acts.tile([P, 6, 512], BF16, tag="eq", bufs=4, align_bytes=64)
-            nc.sync.dma_start(out=eq[:, :, 16:512], in_=hid_rows[:, 6 * bp : 6 * bp + 6, 15:511])
-            eq_t[bp] = eq
+        def load_eq(g):
+            eq = acts.tile([P, 6, 512], BF16, tag="eq", bufs=GROUPS, align_bytes=64)
+            nc.sync.dma_start(out=eq[:, :, 16:512], in_=hidden_rows[:, 6 * g : 6 * g + 6, 15:511])
+            eq_sb[g] = eq
 
-        def load_inv(bp):
+        def heads(g):
+            nc.vector.tensor_copy(out=eq_sb[g][:, :, 1:16], in_=head_hidden[:, 6 * g : 6 * g + 6, 0:15])
+            nc.vector.tensor_copy(out=eq_sb[g][:, :, 0:1], in_=head_input[:, 6 * g : 6 * g + 6].unsqueeze(2))
+
+        def load_inv(g):
             iv = acts.tile([P, 2, 1536], BF16, tag="inv", align_bytes=64)
-            nc.sync.dma_start(out=iv[:, :, 0:512], in_=ii_rows[:, 2 * bp : 2 * bp + 2, :])
-            nc.sync.dma_start(out=iv[:, :, 512:1536], in_=ih_rows[:, 2 * bp : 2 * bp + 2, :])
-            inv_t[bp] = iv
+            nc.sync.dma_start(out=iv[:, :, 0:512], in_=input_rows[:, 2 * g : 2 * g + 2, :])
+            nc.sync.dma_start(out=iv[:, :, 512:1536], in_=state_rows[:, 2 * g : 2 * g + 2, :])
+            inv_sb[g] = iv
 
-        def load_w(w, hh):
-            raw = wst.tile([P, 4, 512], BF16, tag="raw", bufs=5)
+        def load_w(w, half):
+            raw = stage.tile([P, 4, 512], BF16, tag="raw", bufs=5)
             for u in range(2):
                 nc.sync.dma_start(
                     out=raw[:, 2 * u : 2 * u + 2, :],
-                    in_=w_src[w][256 * u : 256 * u + 256, 512 * hh : 512 * hh + 512].rearrange("(p e) c -> p e c", e=2),
+                    in_=w_hbm[w][256 * u : 256 * u + 256, 512 * half : 512 * half + 512].rearrange(
+                        "(p e) c -> p e c", e=2
+                    ),
                 )
-            raw_t[(w, hh)] = raw
+            w_raw[(w, half)] = raw
 
-        def heads(bp):
-            nc.vector.tensor_copy(out=eq_t[bp][:, :, 1:16], in_=head_h[:, 6 * bp : 6 * bp + 6, 0:15])
-            nc.vector.tensor_copy(out=eq_t[bp][:, :, 0:1], in_=head_i[:, 6 * bp : 6 * bp + 6].unsqueeze(2))
-
-        def grouped4(ap):
-            return ap.rearrange("p (b u e) -> p b u e", u=2, e=2)
-
-        def eq_bank(bp, j, pool=tp, tag="tp"):
-            eq_w = eq_t[bp][:].bitcast(F32)
-            bank = pool.tile([P, 2, 2, P], F32, tag=tag)
-            for u in range(2):
-                for t in range(2):
-                    nc.tensor.transpose(bank[:, u, t, :], eq_w[:, 3 * t + j, 128 * u : 128 * u + 128], ident[:])
-            banks[("eq", bp, j)] = bank[:].bitcast(BF16).rearrange("p u t (b e) -> p (t b) u e", e=2)
-
-        def inv_bank(bp, g):
-            inv_w = inv_t[bp][:].bitcast(F32)
-            bank = tp.tile([P, 2, 2, P], F32, tag="tp")
-            for u in range(2):
-                for t in range(2):
-                    lo = 256 * g + 128 * u
-                    nc.tensor.transpose(bank[:, u, t, :], inv_w[:, t, lo : lo + 128], ident[:])
-            banks[("inv", bp, g)] = bank[:].rearrange("p u t b -> p (t b) u")
-
-        def square(bp, j):
-            s = work.tile([P, 1024], F32, tag="sq%d" % j)
-            nc.scalar.activation(out=grouped4(s[:]), in_=banks[("eq", bp, j)], func=ACT.Square)
-            sqs[(bp, j)] = s
-
-        def eq_add(eng, bp, j):
-            eng.tensor_tensor(out=sqs[(bp, 0)][:], in0=sqs[(bp, 0)][:], in1=sqs[(bp, j)][:], op=ALU.add)
-
-        def reciprocal(bp):
-            nc.scalar.activation(
-                out=sqs[(bp, 1)][:], in_=sqs[(bp, 0)][:], func=ACT.Abs_reciprocal_sqrt, bias=eps_t[:]
+        def regroup_w(w, half):
+            grouped = stage.tile([P, 512, 4], BF16, tag="grouped", align_bytes=64)
+            nc.vector.tensor_copy(
+                out=grouped[:].rearrange("p (c i) t -> p c t i", i=4),
+                in_=w_raw[(w, half)][:].rearrange("p t (c i) -> p c t i", i=4),
             )
-            y = work.tile([P, 1024], F32, tag="y1", bufs=3)
-            nc.scalar.activation(out=y[:], in_=sqs[(bp, 1)][:], func=ACT.Square)
-            recip[bp] = y
+            w_grouped[(w, half)] = grouped
 
-        def x_mul(bp, j):
-            gx = work.tile([P, 1024], BF16, tag="gx", bufs=3, align_bytes=64)
-            nc.vector.tensor_tensor(
-                out=grouped4(gx[:]), in0=banks[("eq", bp, j)], in1=grouped4(recip[bp][:]), op=ALU.mult
-            )
-            gxs[(bp, j)] = gx
-
-        def x_quant(bp, j):
-            cols = slice(256 * bp, 256 * bp + 256)
-            nc.vector.quantize_mx(
-                out=x_codes[:, j, cols].bitcast(FP8X4), scales=x_scales[:, j, cols], in_=gxs[(bp, j)][:]
-            )
-
-        def i_copy(bp, g):
-            gi = work.tile([P, 1024], BF16, tag="gi", bufs=3, align_bytes=64)
-            nc.scalar.copy(out=gi[:].bitcast(F32).rearrange("p (b u) -> p b u", u=2), in_=banks[("inv", bp, g)])
-            gis[(bp, g)] = gi
-
-        def i_quant(bp, g):
-            cols = slice(256 * bp, 256 * bp + 256)
-            nc.vector.quantize_mx(
-                out=i_codes[:, g, cols].bitcast(FP8X4), scales=i_scales[:, g, cols], in_=gis[(bp, g)][:]
-            )
-
-        def w_regroup(w, hh):
-            on_scalar = (w, hh) == (WI + 2, 0)
-            grp = wst.tile([P, 512, 4], BF16, tag=("grs" if on_scalar else "grp"), bufs=(1 if on_scalar else 2), align_bytes=64)
-            dst = grp[:].rearrange("p (c i) t -> p c t i", i=4)
-            src = raw_t[(w, hh)][:].rearrange("p t (c i) -> p c t i", i=4)
-            if on_scalar:
-                nc.scalar.copy(out=dst, in_=src)
-            else:
-                nc.vector.tensor_copy(out=dst, in_=src)
-            grp_t[(w, hh)] = grp
-
-        def w_quant(w, hh):
-            cols = slice(512 * hh, 512 * hh + 512)
+        def quantise_w(w, half):
+            cols = slice(512 * half, 512 * half + 512)
             nc.vector.quantize_mx(
                 out=w_codes[:, w, cols].bitcast(FP8X4),
                 scales=w_scales[:, w, cols],
-                in_=grp_t[(w, hh)][:].rearrange("p c t -> p (c t)"),
+                in_=w_grouped[(w, half)][:].rearrange("p c t -> p (c t)"),
             )
 
-        def mx(acc, w, hp, hl, a_codes, a_scales, row, bp, start, stop):
-            hcols = slice(256 * hp + 128 * hl, 256 * hp + 128 * hl + 128)
-            bcols = slice(256 * bp, 256 * bp + 256)
+        def by_word(ap):
+            return ap.rearrange("p (b u e) -> p b u e", u=2, e=2)
+
+        def eq_bank(g, j, pool=ahead, tag="ahead"):
+            words = eq_sb[g][:].bitcast(F32)
+            bank = pool.tile([P, 2, 2, P], F32, tag=tag)
+            for u in range(2):
+                for s in range(2):
+                    nc.tensor.transpose(bank[:, u, s, :], words[:, 3 * s + j, 128 * u : 128 * u + 128], ident[:])
+            banks[("eq", g, j)] = bank[:].bitcast(BF16).rearrange("p u s (b e) -> p (s b) u e", e=2)
+
+        def square(g, j):
+            sq = work.tile([P, 1024], F32, tag="square%d" % j)
+            nc.scalar.activation(out=by_word(sq[:]), in_=banks[("eq", g, j)], func=ACT.Square)
+            squares[(g, j)] = sq
+
+        def add_square(engine, g, j):
+            engine.tensor_tensor(out=squares[(g, 0)][:], in0=squares[(g, 0)][:], in1=squares[(g, j)][:], op=ALU.add)
+
+        def reciprocal(g):
+            nc.scalar.activation(
+                out=squares[(g, 1)][:], in_=squares[(g, 0)][:], func=ACT.Abs_reciprocal_sqrt, bias=eps[:]
+            )
+            r = work.tile([P, 1024], F32, tag="recip", bufs=3)
+            nc.scalar.activation(out=r[:], in_=squares[(g, 1)][:], func=ACT.Square)
+            recip[g] = r
+
+        def scale_eq(g, j):
+            xg = work.tile([P, 1024], BF16, tag="x_grouped", bufs=3, align_bytes=64)
+            nc.vector.tensor_tensor(
+                out=by_word(xg[:]), in0=banks[("eq", g, j)], in1=by_word(recip[g][:]), op=ALU.mult
+            )
+            x_grouped[(g, j)] = xg
+
+        def quantise_x(g, j):
+            cols = slice(256 * g, 256 * g + 256)
+            nc.vector.quantize_mx(
+                out=x_codes[:, j, cols].bitcast(FP8X4), scales=x_scales[:, j, cols], in_=x_grouped[(g, j)][:]
+            )
+
+        def inv_bank(g, k):
+            words = inv_sb[g][:].bitcast(F32)
+            bank = ahead.tile([P, 2, 2, P], F32, tag="ahead")
+            for u in range(2):
+                for s in range(2):
+                    lo = 256 * k + 128 * u
+                    nc.tensor.transpose(bank[:, u, s, :], words[:, s, lo : lo + 128], ident[:])
+            banks[("inv", g, k)] = bank[:].rearrange("p u s b -> p (s b) u")
+
+        def copy_inv(g, k):
+            ig = work.tile([P, 1024], BF16, tag="i_grouped", bufs=3, align_bytes=64)
+            nc.scalar.copy(out=ig[:].bitcast(F32).rearrange("p (b u) -> p b u", u=2), in_=banks[("inv", g, k)])
+            i_grouped[(g, k)] = ig
+
+        def quantise_inv(g, k):
+            cols = slice(256 * g, 256 * g + 256)
+            nc.vector.quantize_mx(
+                out=i_codes[:, k, cols].bitcast(FP8X4), scales=i_scales[:, k, cols], in_=i_grouped[(g, k)][:]
+            )
+
+        def mx(acc, w, h_tile, codes, scales, row, g, start, stop):
+            h_cols = slice(128 * h_tile, 128 * h_tile + 128)
+            b_cols = slice(256 * g, 256 * g + 256)
             nc.tensor.matmul_mx(
                 out=acc,
-                lhsT=w_codes[:, w, hcols].bitcast(FP8X4),
-                lhsT_scale=w_scales[:, w, hcols],
-                rhs=a_codes[:, row, bcols].bitcast(FP8X4),
-                rhs_scale=a_scales[:, row, bcols],
+                lhsT=w_codes[:, w, h_cols].bitcast(FP8X4),
+                lhsT_scale=w_scales[:, w, h_cols],
+                rhs=codes[:, row, b_cols].bitcast(FP8X4),
+                rhs_scale=scales[:, row, b_cols],
                 start=start,
                 stop=stop,
             )
 
-        def products(u):
-            bp, hp = u // 4, u % 4
-            rcs = []
+        def products(r):
+            g, quarter = r // 4, r % 4
+            copies = []
             for j in range(3):
-                right = mm.tile([P, 2, 256], F32, tag="mm")
-                for hl in range(2):
-                    mx(right[:, hl, :], WR, hp, hl, x_codes, x_scales, j, bp, True, True)
-                rc = ep.tile([P, 2, 256], F32, tag="rc", bufs=4)
-                nc.scalar.copy(out=rc[:], in_=right[:])
-                rcs.append(rc)
+                right = ring.tile([P, 2, 256], F32, tag="ring")
+                for i in range(2):
+                    mx(right[:, i, :], W_R, 2 * quarter + i, x_codes, x_scales, j, g, True, True)
+                right_sb = block.tile([P, 2, 256], F32, tag="right", bufs=4)
+                nc.scalar.copy(out=right_sb[:], in_=right[:])
+                copies.append(right_sb)
             for j in range(3):
-                rc = rcs[j]
-                left = mm.tile([P, 2, 256], F32, tag="mm")
-                for hl in range(2):
-                    mx(left[:, hl, :], WL, hp, hl, x_codes, x_scales, j, bp, True, True)
-                p = ep.tile([P, 2, 256], F32, tag="p%d" % j, bufs=6)
-                nc.vector.tensor_tensor(out=p[:], in0=left[:], in1=rc[:], op=ALU.mult)
-                prods[(u, j)] = p
+                left = ring.tile([P, 2, 256], F32, tag="ring")
+                for i in range(2):
+                    mx(left[:, i, :], W_L, 2 * quarter + i, x_codes, x_scales, j, g, True, True)
+                term = block.tile([P, 2, 256], F32, tag="term%d" % j, bufs=6)
+                nc.vector.tensor_tensor(out=term[:], in0=left[:], in1=copies[j][:], op=ALU.mult)
+                terms[(r, j)] = term
 
-        def linear(u):
-            bp, hp = u // 4, u % 4
-            lin = mm.tile([P, 2, 256], F32, tag="mm")
-            for hl in range(2):
-                for g in range(3):
-                    mx(lin[:, hl, :], WI + g, hp, hl, i_codes, i_scales, g, bp, g == 0, g == 2)
-            for hl in range(2):
+        def linear(r):
+            g, quarter = r // 4, r % 4
+            lin = ring.tile([P, 2, 256], F32, tag="ring")
+            for i in range(2):
+                for k in range(3):
+                    mx(lin[:, i, :], W_I + k, 2 * quarter + i, i_codes, i_scales, k, g, k == 0, k == 2)
+            for i in range(2):
                 nc.vector.scalar_tensor_tensor(
-                    out=prods[(u, 0)][:, hl, :],
-                    in0=lin[:, hl, :],
-                    scalar=bias_t[:, 2 * hp + hl : 2 * hp + hl + 1],
-                    in1=prods[(u, 0)][:, hl, :],
+                    out=terms[(r, 0)][:, i, :],
+                    in0=lin[:, i, :],
+                    scalar=bias[:, 2 * quarter + i : 2 * quarter + i + 1],
+                    in1=terms[(r, 0)][:, i, :],
                     op0=ALU.add,
                     op1=ALU.add,
                 )
 
-        def pair_add(u):
-            if u >= PE_ADDS:
-                nc.gpsimd.tensor_tensor(out=prods[(u, 1)][:], in0=prods[(u, 1)][:], in1=prods[(u, 2)][:], op=ALU.add)
-
-        def last_add(u):
-            if u >= PE_ADDS:
-                nc.gpsimd.tensor_tensor(out=prods[(u, 0)][:], in0=prods[(u, 0)][:], in1=prods[(u, 1)][:], op=ALU.add)
-
-        def turn_back(u):
-            o = mm.tile([P, 2, 2, P], F32, tag="mm")
-            terms = 3 if u < PE_ADDS else 1
-            for t in range(2):
-                for hl in range(2):
-                    for i in range(terms):
+        def turn_back(r):
+            bank = ring.tile([P, 2, 2, P], F32, tag="ring")
+            for s in range(2):
+                for i in range(2):
+                    for j in range(3):
                         nc.tensor.matmul(
-                            out=o[:, t, hl, :],
-                            lhsT=prods[(u, i)][:, hl, 128 * t : 128 * t + 128],
+                            out=bank[:, s, i, :],
+                            lhsT=terms[(r, j)][:, i, 128 * s : 128 * s + 128],
                             rhs=ident[:],
                             is_transpose=True,
-                            start=(i == 0),
-                            stop=(i == terms - 1),
+                            start=(j == 0),
+                            stop=(j == 2),
                         )
-            outs[u] = o
+            turned[r] = bank
 
-        def finish(u):
-            bp, hp = u // 4, u % 4
-            res = ep.tile([P, 2, 256], F32, tag="res")
-            nc.scalar.activation(out=res[:], in_=outs[u][:].rearrange("p t l h -> p t (l h)"), func=ACT.Tanh)
-            nc.sync.dma_start(out=out_rows[:, 2 * bp : 2 * bp + 2, 256 * hp : 256 * hp + 256], in_=res[:])
+        def finish(r):
+            g, quarter = r // 4, r % 4
+            res = block.tile([P, 2, 256], F32, tag="res")
+            nc.scalar.activation(out=res[:], in_=turned[r][:].rearrange("p s i h -> p s (i h)"), func=ACT.Tanh)
+            nc.sync.dma_start(out=out_rows[:, 2 * g : 2 * g + 2, 256 * quarter : 256 * quarter + 256], in_=res[:])
 
         with nc.allow_non_contiguous_dma(reason="the first 16 channels arrive in short runs"):
-            nc.scalar.dma_start(out=head_i[:], in_=equivariant_input.rearrange("(p t) j -> p (t j)", t=8))
-            nc.scalar.dma_start(out=head_h[:, 0:6, 0:15], in_=hid_rows[:, 0:6, 0:15])
-            nc.scalar.dma_start(out=head_h[:, 6:24, 0:15], in_=hid_rows[:, 6:24, 0:15])
+            nc.scalar.dma_start(out=head_input[:], in_=equivariant_input.rearrange("(p s) j -> p (s j)", s=8))
+            nc.scalar.dma_start(out=head_hidden[:, 0:6, 0:15], in_=hidden_rows[:, 0:6, 0:15])
+            nc.scalar.dma_start(out=head_hidden[:, 6:24, 0:15], in_=hidden_rows[:, 6:24, 0:15])
         nc.vector.memset(bias_rows[:], 0.0)
         nc.gpsimd.dma_start(out=bias_rows[0:8, :], in_=b_ii.rearrange("(r c) -> r c", c=P))
         load_eq(0)
-        load_w(WR, 0)
-        load_w(WL, 0)
+        load_w(W_R, 0)
+        load_w(W_L, 0)
         load_eq(1)
-        load_w(WI, 0)
+        load_w(W_I, 0)
         load_inv(0)
-        load_w(WI + 1, 0)
-        load_w(WI + 2, 0)
+        load_w(W_I + 1, 0)
+        load_w(W_I + 2, 0)
         load_eq(2)
         load_eq(3)
         load_inv(1)
@@ -273,102 +264,104 @@ def tile_ryeelman_pa_kernel(
         heads(0)
         for j in range(3):
             eq_bank(0, j)
-        w_regroup(WR, 0)
-        w_regroup(WL, 0)
+        for w in (W_R, W_L):
+            regroup_w(w, 0)
         for j in range(3):
             square(0, j)
             if j:
-                eq_add(nc.vector, 0, j)
+                add_square(nc.vector, 0, j)
         reciprocal(0)
-        for w in (WR, WL):
-            w_quant(w, 0)
+        for w in (W_R, W_L):
+            quantise_w(w, 0)
             load_w(w, 1)
         heads(1)
-        bias_ps = mm.tile([P, P], BF16, tag="mm")
-        nc.tensor.transpose(bias_ps[:], bias_rows[:], ident_b[:])
-        nc.vector.tensor_copy(out=bias_t[:], in_=bias_ps[:, 0:8])
+        bias_ps = ring.tile([P, P], BF16, tag="ring")
+        nc.tensor.transpose(bias_ps[:], bias_rows[:], ident_bf[:])
+        nc.vector.tensor_copy(out=bias[:], in_=bias_ps[:, 0:8])
         heads(2)
         heads(3)
         for j in range(3):
             eq_bank(0, j)
         for j in range(3):
-            eq_bank(1, j, mm, "mm")
+            eq_bank(1, j, ring, "ring")
         for j in range(3):
-            x_mul(0, j)
-            x_quant(0, j)
+            scale_eq(0, j)
+            quantise_x(0, j)
             square(1, j)
         for j in (1, 2):
-            eq_add(nc.vector, 1, j)
+            add_square(nc.vector, 1, j)
 
-        def banks_for(u):
-            bp, hp = u // 4, u % 4
-            if hp == 0 and bp < 4:
-                for g in range(3):
-                    inv_bank(bp, g)
-            if u in (1, 2):
+        def banks_for(r):
+            g, quarter = r // 4, r % 4
+            if quarter == 0 and g < GROUPS:
+                for k in range(3):
+                    inv_bank(g, k)
+            if r in (1, 2):
                 for j in range(3):
-                    eq_bank(u + 1, j)
-            if u == 3:
+                    eq_bank(r + 1, j)
+            if r == 3:
                 for j in range(3):
                     eq_bank(1, j)
-            if 1 <= bp < 3 and hp:
-                eq_bank(bp + 1, hp - 1)
+            if 1 <= g < GROUPS - 1 and quarter:
+                eq_bank(g + 1, quarter - 1)
 
-        def side(u):
-            bp, hp = u // 4, u % 4
-            if hp == 0 and bp < 4:
-                for g in range(3):
-                    i_copy(bp, g)
-            if u < 3:
-                hh = 0 if u == 0 else 1
-                for w in ((WI, WI + 1, WI + 2), (WR, WL), (WI, WI + 1, WI + 2))[u]:
-                    w_regroup(w, hh)
-                    w_quant(w, hh)
-                    if hh == 0:
-                        load_w(w, 1)
-            if u == 0:
+        def before_products(r):
+            g, quarter = r // 4, r % 4
+            if 1 <= g < GROUPS - 1 and quarter:
+                scale_eq(g + 1, quarter - 1)
+                quantise_x(g + 1, quarter - 1)
+
+        def side_work(r):
+            g, quarter = r // 4, r % 4
+            if quarter == 0 and g < GROUPS:
+                for k in range(3):
+                    copy_inv(g, k)
+            if r == 0:
+                for k in range(3):
+                    regroup_w(W_I + k, 0)
+                    quantise_w(W_I + k, 0)
+                    load_w(W_I + k, 1)
                 load_inv(2)
                 load_inv(3)
                 reciprocal(1)
-            if hp == 0 and bp < 4:
-                for g in range(3):
-                    i_quant(bp, g)
-            if u in (1, 2):
+            if r == 1:
+                for w in (W_R, W_L):
+                    regroup_w(w, 1)
+                    quantise_w(w, 1)
+            if r == 2:
+                for k in range(3):
+                    regroup_w(W_I + k, 1)
+                    quantise_w(W_I + k, 1)
+            if quarter == 0 and g < GROUPS:
+                for k in range(3):
+                    quantise_inv(g, k)
+            if r in (1, 2):
                 for j in range(3):
-                    square(u + 1, j)
+                    square(r + 1, j)
                     if j:
-                        eq_add(nc.gpsimd, u + 1, j)
-            if u in (2, 3):
-                reciprocal(u)
-            if u == 3:
+                        add_square(nc.gpsimd, r + 1, j)
+            if r in (2, 3):
+                reciprocal(r)
+            if r == 3:
                 for j in range(3):
-                    x_mul(1, j)
-                    if j:
-                        x_quant(1, j - 1)
-                x_quant(1, 2)
+                    scale_eq(1, j)
+                    quantise_x(1, j)
 
-        def early(u):
-            bp, hp = u // 4, u % 4
-            if 1 <= bp < 3 and hp:
-                x_mul(bp + 1, hp - 1)
-                x_quant(bp + 1, hp - 1)
-
-        for u in range(18):
-            early(u)
-            if u < 16:
-                products(u)
-                pair_add(u)
-            if u == 0:
+        for r in range(ROUNDS + 2):
+            before_products(r)
+            if r < ROUNDS:
+                products(r)
+            if r == 0:
                 banks_for(0)
-            if 1 <= u < 17:
-                linear(u - 1)
-                last_add(u - 1)
-            side(u)
-            done = [v for v in range(16) if max(v + 2, 3 + v // 2) == u]
-            for v in done:
+            if 1 <= r <= ROUNDS:
+                linear(r - 1)
+            side_work(r)
+            due = [v for v in range(ROUNDS) if max(v + 2, 3 + v // 2) == r]
+            for v in due[:-1]:
                 turn_back(v)
-                if v != done[-1]:
-                    finish(v)
-            banks_for(u + 1)
-            if done:
-                finish(done[-1])
+                finish(v)
+            for v in due[-1:]:
+                turn_back(v)
+            banks_for(r + 1)
+            for v in due[-1:]:
+                finish(v)

@@ -222,18 +222,26 @@ def tile_ryeelman_pa_kernel(
                     op1=ALU.add,
                 )
 
+        def tensor_adds(r):
+            return r < 4 or r >= ROUNDS - 2
+
+        def add_terms(r, j):
+            if not tensor_adds(r):
+                nc.gpsimd.tensor_tensor(out=terms[(r, j - 1)][:], in0=terms[(r, j - 1)][:], in1=terms[(r, j)][:], op=ALU.add)
+
         def turn_back(r):
             bank = ring.tile([P, 2, 2, P], F32, tag="ring")
+            n_terms = 3 if tensor_adds(r) else 1
             for s in range(2):
                 for i in range(2):
-                    for j in range(3):
+                    for j in range(n_terms):
                         nc.tensor.matmul(
                             out=bank[:, s, i, :],
                             lhsT=terms[(r, j)][:, i, 128 * s : 128 * s + 128],
                             rhs=ident[:],
                             is_transpose=True,
                             start=(j == 0),
-                            stop=(j == 2),
+                            stop=(j == n_terms - 1),
                         )
             turned[r] = bank
 
@@ -351,10 +359,12 @@ def tile_ryeelman_pa_kernel(
             before_products(r)
             if r < ROUNDS:
                 products(r)
+                add_terms(r, 2)
             if r == 0:
                 banks_for(0)
             if 1 <= r <= ROUNDS:
                 linear(r - 1)
+                add_terms(r - 1, 1)
             side_work(r)
             due = [v for v in range(ROUNDS) if max(v + 2, 3 + v // 2) == r]
             for v in due[:-1]:

@@ -33,7 +33,6 @@ def tile_ryeelman_pa_kernel(
 ):
     nc = tc.nc
     with ExitStack() as ctx:
-        ctx.enter_context(tc.manual_schedule())
         keep = ctx.enter_context(tc.tile_pool(name="keep", bufs=1))
         acts = ctx.enter_context(tc.tile_pool(name="acts", bufs=3))
         work = ctx.enter_context(tc.tile_pool(name="work", bufs=2))

@@ -38,8 +38,8 @@ def tile_ryeelman_pa_kernel(
         work = ctx.enter_context(tc.tile_pool(name="work", bufs=2))
         stage = ctx.enter_context(tc.tile_pool(name="stage", bufs=2))
         block = ctx.enter_context(tc.tile_pool(name="block", bufs=3))
-        ahead = ctx.enter_context(tc.psum_pool(name="ahead", bufs=3))
-        ring = ctx.enter_context(tc.psum_pool(name="ring", bufs=5))
+        ahead = ctx.enter_context(tc.psum_pool(name="ahead", bufs=2))
+        ring = ctx.enter_context(tc.psum_pool(name="ring", bufs=6))
 
         zero = keep.tile([P, 1], F32)
         nc.vector.memset(zero[:], 0.0)
@@ -74,7 +74,14 @@ def tile_ryeelman_pa_kernel(
 
         def load_eq(g):
             eq = acts.tile([P, 6, 512], BF16, tag="eq", bufs=GROUPS, align_bytes=64)
-            nc.sync.dma_start(out=eq[:, :, 16:512], in_=hidden_rows[:, 6 * g : 6 * g + 6, 15:511])
+            if g == 0:
+                for j in range(3):
+                    nc.sync.dma_start(
+                        out=eq[:].rearrange("p (s j) c -> p s j c", j=3)[:, :, j, 16:512],
+                        in_=hidden_rows[:, 0:6, :].rearrange("p (s j) c -> p s j c", j=3)[:, :, j, 15:511],
+                    )
+            else:
+                nc.sync.dma_start(out=eq[:, :, 16:512], in_=hidden_rows[:, 6 * g : 6 * g + 6, 15:511])
             eq_sb[g] = eq
 
         def heads(g):
@@ -99,7 +106,7 @@ def tile_ryeelman_pa_kernel(
             w_raw[(w, half)] = raw
 
         def regroup_w(w, half):
-            grouped = stage.tile([P, 512, 4], BF16, tag="grouped", align_bytes=64)
+            grouped = stage.tile([P, 512, 4], BF16, tag="grouped", bufs=3, align_bytes=64)
             nc.vector.tensor_copy(
                 out=grouped[:].rearrange("p (c i) t -> p c t i", i=4),
                 in_=w_raw[(w, half)][:].rearrange("p t (c i) -> p c t i", i=4),
@@ -194,7 +201,7 @@ def tile_ryeelman_pa_kernel(
                 right = ring.tile([P, 2, 256], F32, tag="ring")
                 for i in range(2):
                     mx(right[:, i, :], W_R, 2 * quarter + i, x_codes, x_scales, j, g, True, True)
-                right_sb = block.tile([P, 2, 256], F32, tag="right", bufs=4)
+                right_sb = block.tile([P, 2, 256], F32, tag="right", bufs=6)
                 nc.scalar.copy(out=right_sb[:], in_=right[:])
                 copies.append(right_sb)
             for j in range(3):
@@ -251,13 +258,13 @@ def tile_ryeelman_pa_kernel(
             nc.sync.dma_start(out=out_rows[:, 2 * g : 2 * g + 2, 256 * quarter : 256 * quarter + 256], in_=res[:])
 
         with nc.allow_non_contiguous_dma(reason="the first 16 channels arrive in short runs"):
-            nc.scalar.dma_start(out=head_input[:], in_=equivariant_input.rearrange("(p s) j -> p (s j)", s=8))
-            nc.scalar.dma_start(out=head_hidden[:, 0:6, 0:15], in_=hidden_rows[:, 0:6, 0:15])
+            nc.sync.dma_start(out=head_input[:], in_=equivariant_input.rearrange("(p s) j -> p (s j)", s=8))
+            nc.sync.dma_start(out=head_hidden[:, 0:6, 0:15], in_=hidden_rows[:, 0:6, 0:15])
             nc.scalar.dma_start(out=head_hidden[:, 6:24, 0:15], in_=hidden_rows[:, 6:24, 0:15])
         nc.vector.memset(bias_rows[:], 0.0)
         nc.gpsimd.dma_start(out=bias_rows[0:8, :], in_=b_ii.rearrange("(r c) -> r c", c=P))
-        load_eq(0)
         load_w(W_R, 0)
+        load_eq(0)
         load_w(W_L, 0)
         load_eq(1)
         load_w(W_I, 0)

from contextlib import ExitStack

import concourse.mybir as mybir
from concourse.masks import make_identity

F32 = mybir.dt.float32
BF16 = mybir.dt.bfloat16
U32 = mybir.dt.uint32
U8 = mybir.dt.uint8
FP8X4 = mybir.dt.float8_e4m3fn_x4
ACT = mybir.ActivationFunctionType
ALU = mybir.AluOpType

FLOPS = 2 * (2 * 3072 * 512 * 1024 + 1024 * 1536 * 1024)
EPS = 1e-6
P = 128
GROUPS = 4
ROUNDS = 16
W_R, W_L, W_I = 0, 1, 2


def tile_ryeelman_pa_kernel(
    tc,
    invariant_input,
    equivariant_input,
    invariant_hidden,
    equivariant_hidden,
    W_left,
    W_right,
    W_ii,
    b_ii,
    out,
):
    nc = tc.nc
    with ExitStack() as ctx:
        keep = ctx.enter_context(tc.tile_pool(name="keep", bufs=1))
        acts = ctx.enter_context(tc.tile_pool(name="acts", bufs=3))
        work = ctx.enter_context(tc.tile_pool(name="work", bufs=2))
        stage = ctx.enter_context(tc.tile_pool(name="stage", bufs=2))
        block = ctx.enter_context(tc.tile_pool(name="block", bufs=3))
        ahead = ctx.enter_context(tc.psum_pool(name="ahead", bufs=2))
        ring = ctx.enter_context(tc.psum_pool(name="ring", bufs=6))

        zero = keep.tile([P, 1], F32)
        nc.vector.memset(zero[:], 0.0)
        eps = keep.tile([P, 1], F32)
        nc.vector.tensor_scalar_add(out=eps[:], in0=zero[:], scalar1=EPS)
        warm = keep.tile([P, 1], F32)
        nc.scalar.activation(out=warm[:], in_=eps[:], func=ACT.Abs_reciprocal_sqrt)
        ident = keep.tile([P, P], F32)
        make_identity(nc, ident[:])
        ident_bf = keep.tile([P, P], BF16)
        make_identity(nc, ident_bf[:])

        head_hidden = keep.tile([P, 24, 16], BF16)
        head_input = keep.tile([P, 24], BF16)
        bias_rows = keep.tile([P, P], BF16)
        bias = keep.tile([P, 8], F32)
        w_codes = keep.tile([P, 5, 1024], U32, align_bytes=64)
        w_scales = keep.tile([P, 5, 1024], U8, align_bytes=64)
        x_codes = keep.tile([P, 3, 1024], U32, align_bytes=64)
        x_scales = keep.tile([P, 3, 1024], U8, align_bytes=64)
        i_codes = keep.tile([P, 3, 1024], U32, align_bytes=64)
        i_scales = keep.tile([P, 3, 1024], U8, align_bytes=64)

        hidden_rows = equivariant_hidden.rearrange("(p s) j c -> p (s j) c", s=8)
        input_rows = invariant_input.rearrange("(p s) c -> p s c", s=8)
        state_rows = invariant_hidden.rearrange("(p s) c -> p s c", s=8)
        out_rows = out.rearrange("(p s) h -> p s h", s=8)
        w_hbm = (W_right, W_left, W_ii[0:512, :], W_ii[512:1024, :], W_ii[1024:1536, :])

        eq_sb, inv_sb, w_raw, w_grouped = {}, {}, {}, {}
        banks, squares, recip, x_grouped, i_grouped, terms, turned = {}, {}, {}, {}, {}, {}, {}

        def load_eq(g):
            eq = acts.tile([P, 6, 512], BF16, tag="eq", bufs=GROUPS, align_bytes=64)
            if g == 0:
                for j in range(3):
                    nc.sync.dma_start(
                        out=eq[:].rearrange("p (s j) c -> p s j c", j=3)[:, :, j, 16:512],
                        in_=hidden_rows[:, 0:6, :].rearrange("p (s j) c -> p s j c", j=3)[:, :, j, 15:511],
                    )
            else:
                nc.sync.dma_start(out=eq[:, :, 16:512], in_=hidden_rows[:, 6 * g : 6 * g + 6, 15:511])
            eq_sb[g] = eq

        def heads(g):
            nc.vector.tensor_copy(out=eq_sb[g][:, :, 1:16], in_=head_hidden[:, 6 * g : 6 * g + 6, 0:15])
            nc.vector.tensor_copy(out=eq_sb[g][:, :, 0:1], in_=head_input[:, 6 * g : 6 * g + 6].unsqueeze(2))

        def load_inv(g):
            iv = acts.tile([P, 2, 1536], BF16, tag="inv", align_bytes=64)
            nc.sync.dma_start(out=iv[:, :, 0:512], in_=input_rows[:, 2 * g : 2 * g + 2, :])
            nc.sync.dma_start(out=iv[:, :, 512:1536], in_=state_rows[:, 2 * g : 2 * g + 2, :])
            inv_sb[g] = iv

        def load_w(w, half):
            raw = stage.tile([P, 4, 512], BF16, tag="raw", bufs=5)
            for u in range(2):
                nc.sync.dma_start(
                    out=raw[:, 2 * u : 2 * u + 2, :],
                    in_=w_hbm[w][256 * u : 256 * u + 256, 512 * half : 512 * half + 512].rearrange(
                        "(p e) c -> p e c", e=2
                    ),
                )
            w_raw[(w, half)] = raw

        def regroup_w(w, half):
            grouped = stage.tile([P, 512, 4], BF16, tag="grouped", bufs=3, align_bytes=64)
            nc.vector.tensor_copy(
                out=grouped[:].rearrange("p (c i) t -> p c t i", i=4),
                in_=w_raw[(w, half)][:].rearrange("p t (c i) -> p c t i", i=4),
            )
            w_grouped[(w, half)] = grouped

        def quantise_w(w, half):
            cols = slice(512 * half, 512 * half + 512)
            nc.vector.quantize_mx(
                out=w_codes[:, w, cols].bitcast(FP8X4),
                scales=w_scales[:, w, cols],
                in_=w_grouped[(w, half)][:].rearrange("p c t -> p (c t)"),
            )

        def by_word(ap):
            return ap.rearrange("p (b u e) -> p b u e", u=2, e=2)

        def eq_bank(g, j, pool=ahead, tag="ahead"):
            words = eq_sb[g][:].bitcast(F32)
            bank = pool.tile([P, 2, 2, P], F32, tag=tag)
            for u in range(2):
                for s in range(2):
                    nc.tensor.transpose(bank[:, u, s, :], words[:, 3 * s + j, 128 * u : 128 * u + 128], ident[:])
            banks[("eq", g, j)] = bank[:].bitcast(BF16).rearrange("p u s (b e) -> p (s b) u e", e=2)

        def square(g, j):
            sq = work.tile([P, 1024], F32, tag="square%d" % j)
            nc.scalar.activation(out=by_word(sq[:]), in_=banks[("eq", g, j)], func=ACT.Square)
            squares[(g, j)] = sq

        def add_square(engine, g, j):
            engine.tensor_tensor(out=squares[(g, 0)][:], in0=squares[(g, 0)][:], in1=squares[(g, j)][:], op=ALU.add)

        def reciprocal(g):
            nc.scalar.activation(
                out=squares[(g, 1)][:], in_=squares[(g, 0)][:], func=ACT.Abs_reciprocal_sqrt, bias=eps[:]
            )
            r = work.tile([P, 1024], F32, tag="recip", bufs=3)
            nc.scalar.activation(out=r[:], in_=squares[(g, 1)][:], func=ACT.Square)
            recip[g] = r

        def scale_eq(g, j):
            xg = work.tile([P, 1024], BF16, tag="x_grouped", bufs=3, align_bytes=64)
            nc.vector.tensor_tensor(
                out=by_word(xg[:]), in0=banks[("eq", g, j)], in1=by_word(recip[g][:]), op=ALU.mult
            )
            x_grouped[(g, j)] = xg

        def quantise_x(g, j):
            cols = slice(256 * g, 256 * g + 256)
            nc.vector.quantize_mx(
                out=x_codes[:, j, cols].bitcast(FP8X4), scales=x_scales[:, j, cols], in_=x_grouped[(g, j)][:]
            )

        def inv_bank(g, k):
            words = inv_sb[g][:].bitcast(F32)
            bank = ahead.tile([P, 2, 2, P], F32, tag="ahead")
            for u in range(2):
                for s in range(2):
                    lo = 256 * k + 128 * u
                    nc.tensor.transpose(bank[:, u, s, :], words[:, s, lo : lo + 128], ident[:])
            banks[("inv", g, k)] = bank[:].rearrange("p u s b -> p (s b) u")

        def copy_inv(g, k):
            ig = work.tile([P, 1024], BF16, tag="i_grouped", bufs=3, align_bytes=64)
            nc.scalar.copy(out=ig[:].bitcast(F32).rearrange("p (b u) -> p b u", u=2), in_=banks[("inv", g, k)])
            i_grouped[(g, k)] = ig

        def quantise_inv(g, k):
            cols = slice(256 * g, 256 * g + 256)
            nc.vector.quantize_mx(
                out=i_codes[:, k, cols].bitcast(FP8X4), scales=i_scales[:, k, cols], in_=i_grouped[(g, k)][:]
            )

        def mx(acc, w, h_tile, codes, scales, row, g, start, stop):
            h_cols = slice(128 * h_tile, 128 * h_tile + 128)
            b_cols = slice(256 * g, 256 * g + 256)
            nc.tensor.matmul_mx(
                out=acc,
                lhsT=w_codes[:, w, h_cols].bitcast(FP8X4),
                lhsT_scale=w_scales[:, w, h_cols],
                rhs=codes[:, row, b_cols].bitcast(FP8X4),
                rhs_scale=scales[:, row, b_cols],
                start=start,
                stop=stop,
            )

        def products(r):
            g, quarter = r // 4, r % 4
            copies = []
            for j in range(3):
                right = ring.tile([P, 2, 256], F32, tag="ring")
                for i in range(2):
                    mx(right[:, i, :], W_R, 2 * quarter + i, x_codes, x_scales, j, g, True, True)
                right_sb = block.tile([P, 2, 256], F32, tag="right", bufs=6)
                nc.scalar.copy(out=right_sb[:], in_=right[:])
                copies.append(right_sb)
            for j in range(3):
                left = ring.tile([P, 2, 256], F32, tag="ring")
                for i in range(2):
                    mx(left[:, i, :], W_L, 2 * quarter + i, x_codes, x_scales, j, g, True, True)
                term = block.tile([P, 2, 256], F32, tag="term%d" % j, bufs=6)
                nc.vector.tensor_tensor(out=term[:], in0=left[:], in1=copies[j][:], op=ALU.mult)
                terms[(r, j)] = term

        def linear(r):
            g, quarter = r // 4, r % 4
            lin = ring.tile([P, 2, 256], F32, tag="ring")
            for i in range(2):
                for k in range(3):
                    mx(lin[:, i, :], W_I + k, 2 * quarter + i, i_codes, i_scales, k, g, k == 0, k == 2)
            for i in range(2):
                nc.vector.scalar_tensor_tensor(
                    out=terms[(r, 0)][:, i, :],
                    in0=lin[:, i, :],
                    scalar=bias[:, 2 * quarter + i : 2 * quarter + i + 1],
                    in1=terms[(r, 0)][:, i, :],
                    op0=ALU.add,
                    op1=ALU.add,
                )

        def tensor_adds(r):
            return r < 4 or r >= ROUNDS - 2

        def add_terms(r, j):
            if not tensor_adds(r):
                nc.gpsimd.tensor_tensor(out=terms[(r, j - 1)][:], in0=terms[(r, j - 1)][:], in1=terms[(r, j)][:], op=ALU.add)

        def turn_back(r):
            bank = ring.tile([P, 2, 2, P], F32, tag="ring")
            n_terms = 3 if tensor_adds(r) else 1
            for s in range(2):
                for i in range(2):
                    for j in range(n_terms):
                        nc.tensor.matmul(
                            out=bank[:, s, i, :],
                            lhsT=terms[(r, j)][:, i, 128 * s : 128 * s + 128],
                            rhs=ident[:],
                            is_transpose=True,
                            start=(j == 0),
                            stop=(j == n_terms - 1),
                        )
            turned[r] = bank

        def finish(r):
            g, quarter = r // 4, r % 4
            res = block.tile([P, 2, 256], F32, tag="res")
            nc.scalar.activation(out=res[:], in_=turned[r][:].rearrange("p s i h -> p s (i h)"), func=ACT.Tanh)
            nc.sync.dma_start(out=out_rows[:, 2 * g : 2 * g + 2, 256 * quarter : 256 * quarter + 256], in_=res[:])

        with nc.allow_non_contiguous_dma(reason="the first 16 channels arrive in short runs"):
            nc.sync.dma_start(out=head_input[:], in_=equivariant_input.rearrange("(p s) j -> p (s j)", s=8))
            nc.sync.dma_start(out=head_hidden[:, 0:6, 0:15], in_=hidden_rows[:, 0:6, 0:15])
            nc.scalar.dma_start(out=head_hidden[:, 6:24, 0:15], in_=hidden_rows[:, 6:24, 0:15])
        nc.vector.memset(bias_rows[:], 0.0)
        nc.gpsimd.dma_start(out=bias_rows[0:8, :], in_=b_ii.rearrange("(r c) -> r c", c=P))
        load_w(W_R, 0)
        load_eq(0)
        load_w(W_L, 0)
        load_eq(1)
        load_w(W_I, 0)
        load_inv(0)
        load_w(W_I + 1, 0)
        load_w(W_I + 2, 0)
        load_eq(2)
        load_eq(3)
        load_inv(1)

        heads(0)
        for j in range(3):
            eq_bank(0, j)
        for w in (W_R, W_L):
            regroup_w(w, 0)
        for j in range(3):
            square(0, j)
            if j:
                add_square(nc.vector, 0, j)
        reciprocal(0)
        for w in (W_R, W_L):
            quantise_w(w, 0)
            load_w(w, 1)
        heads(1)
        bias_ps = ring.tile([P, P], BF16, tag="ring")
        nc.tensor.transpose(bias_ps[:], bias_rows[:], ident_bf[:])
        nc.vector.tensor_copy(out=bias[:], in_=bias_ps[:, 0:8])
        heads(2)
        heads(3)
        for j in range(3):
            eq_bank(0, j)
        for j in range(3):
            eq_bank(1, j, ring, "ring")
        for j in range(3):
            scale_eq(0, j)
            quantise_x(0, j)
            square(1, j)
        for j in (1, 2):
            add_square(nc.vector, 1, j)

        def banks_for(r):
            g, quarter = r // 4, r % 4
            if quarter == 0 and g < GROUPS:
                for k in range(3):
                    inv_bank(g, k)
            if r in (1, 2):
                for j in range(3):
                    eq_bank(r + 1, j)
            if r == 3:
                for j in range(3):
                    eq_bank(1, j)
            if 1 <= g < GROUPS - 1 and quarter:
                eq_bank(g + 1, quarter - 1)

        def before_products(r):
            g, quarter = r // 4, r % 4
            if 1 <= g < GROUPS - 1 and quarter:
                scale_eq(g + 1, quarter - 1)
                quantise_x(g + 1, quarter - 1)

        def side_work(r):
            g, quarter = r // 4, r % 4
            if quarter == 0 and g < GROUPS:
                for k in range(3):
                    copy_inv(g, k)
            if r == 0:
                for k in range(3):
                    regroup_w(W_I + k, 0)
                    quantise_w(W_I + k, 0)
                    load_w(W_I + k, 1)
                load_inv(2)
                load_inv(3)
                reciprocal(1)
            if r == 1:
                for w in (W_R, W_L):
                    regroup_w(w, 1)
                    quantise_w(w, 1)
            if r == 2:
                for k in range(3):
                    regroup_w(W_I + k, 1)
                    quantise_w(W_I + k, 1)
            if quarter == 0 and g < GROUPS:
                for k in range(3):
                    quantise_inv(g, k)
            if r in (1, 2):
                for j in range(3):
                    square(r + 1, j)
                    if j:
                        add_square(nc.gpsimd, r + 1, j)
            if r in (2, 3):
                reciprocal(r)
            if r == 3:
                for j in range(3):
                    scale_eq(1, j)
                    quantise_x(1, j)

        for r in range(ROUNDS + 2):
            before_products(r)
            if r < ROUNDS:
                products(r)
                add_terms(r, 2)
            if r == 0:
                banks_for(0)
            if 1 <= r <= ROUNDS:
                linear(r - 1)
                add_terms(r - 1, 1)
            side_work(r)
            due = [v for v in range(ROUNDS) if max(v + 2, 3 + v // 2) == r]
            for v in due[:-1]:
                turn_back(v)
                finish(v)
            for v in due[-1:]:
                turn_back(v)
            banks_for(r + 1)
            for v in due[-1:]:
                finish(v)
